import numpy as np
import ml_dtypes


def mxq(x, axis, fmt="e4m3"):
    dtype, down = {"e4m3": (ml_dtypes.float8_e4m3fn, 7), "e5m2": (ml_dtypes.float8_e5m2, 14)}[fmt]
    v = np.moveaxis(np.asarray(x, np.float32).astype(ml_dtypes.bfloat16).astype(np.float64), axis, -1)
    blocks = v.reshape(v.shape[:-1] + (-1, 32))
    amax = np.abs(blocks).max(-1, keepdims=True)
    byte = np.maximum(np.where(amax > 0, np.frexp(amax)[1] - 1 + 127, 0) - down, 1)
    scale = np.exp2(byte - 127.0)
    codes = (blocks / scale).astype(np.float32).astype(dtype).astype(np.float64)
    return np.moveaxis((codes * scale).reshape(v.shape), -1, axis)


WIDE = False


def mx_kscale(k):
    if not WIDE:
        return np.ones(k)
    levels = np.array([20, -20, 10, -10, 0])
    a = np.random.permutation(np.resize(levels, k // 512 * 4)).reshape(k // 512, 4)
    idx = np.arange(k)
    return np.exp2(a[idx // 512, idx % 128 // 32])


BF16 = ml_dtypes.bfloat16


def bf(x):
    return np.asarray(x, np.float32).astype(BF16)


def f64(x):
    return np.asarray(x).astype(np.float64)


T, B, D, U, V, E = 2, 512, 512, 512, 512, 8
G = 2 * E
K = V * E


def softmax(v):
    e = np.exp(v - v.max(-1, keepdims=True))
    return e / e.sum(-1, keepdims=True)


def setup_inputs():
    rn = np.random.standard_normal
    sv = mx_kscale(K)[::E]
    task_h = bf(np.abs(rn((T, B, U))) * 0.55)
    share_h = bf(np.abs(rn((B, U))) * 0.5)
    ews1 = bf(rn((U, V, E)) * 2.0 / np.sqrt(U))
    ebs1 = bf(rn((V, E)) * 0.5)
    ew0 = bf(rn((T, U, V, E)) * 2.0 / np.sqrt(U))
    eb1 = bf(rn((T, V, E)) * 0.5)
    gate_pre1 = bf(rn((T, B, G)))
    gb1 = bf(rn((T, G)) * 0.5)
    g = bf(rn((T, B, V)) * np.exp2(np.random.randint(-12, 1, (T, B, 1))) * 32.0 * sv)
    zt = (f64(task_h) @ f64(ew0).reshape(T, U, K)).reshape(T, B, V, E) + f64(eb1)[:, None]
    gate = softmax(f64(gate_pre1) + f64(gb1)[:, None])
    return {
        "task_h": task_h,
        "share_h": share_h,
        "ews1": ews1,
        "ebs1": ebs1,
        "ew1": bf(f64(ew0) / sv[None, None, :, None]),
        "eb1": eb1,
        "gate_pre1": gate_pre1,
        "gb1": gb1,
        "zt": np.asarray(zt, np.float32),
        "gate": np.asarray(gate, np.float32),
        "grad_out": g,
    }


def reference(task_h, share_h, ews1, ebs1, ew1, eb1, gate_pre1, gb1, zt, gate, grad_out):
    dz = f64(grad_out)[:, :, :, None] * f64(gate)[:, :, None, :E] * (f64(zt) > 0.0)
    dz = dz.reshape(T, B, K)
    w = f64(ew1).reshape(T, U, K)
    return mxq(dz, 2, "e5m2") @ mxq(w, 2, "e4m3").transpose(0, 2, 1)

@@ -1,0 +1,269 @@
+from contextlib import ExitStack
+
+import concourse.mybir as mybir
+from concourse.masks import make_identity
+
+F32 = mybir.dt.float32
+BF16 = mybir.dt.bfloat16
+U32 = mybir.dt.uint32
+U8 = mybir.dt.uint8
+E4M3X4 = mybir.dt.float8_e4m3fn_x4
+E5M2X4 = mybir.dt.float8_e5m2_x4
+ALU = mybir.AluOpType
+
+P = 128
+T, B, U, V, E = 2, 512, 512, 512, 8
+K = V * E
+K_PASS = 4 * P
+PASSES = K // K_PASS
+ROW_TILES = B // P
+TOKEN_TILES = T * ROW_TILES
+WORDS = K // 2
+HALF = K // 2
+
+FLOPS = 2 * T * B * U * K
+BYTES = 4 * T * B * K + 2 * T * U * K + 2 * T * B * V + 4 * T * B * E + 4 * T * B * U
+
+
+def tile_plelayer_pb_v_kernel(
+    tc, task_h, share_h, ews1, ebs1, ew1, eb1, gate_pre1, gb1, zt, gate, grad_out, out
+):
+    nc = tc.nc
+    with ExitStack() as ctx:
+        const = ctx.enter_context(tc.tile_pool(name="const", bufs=1))
+        zt_pool = ctx.enter_context(tc.tile_pool(name="zt", bufs=6))
+        w_pool = ctx.enter_context(tc.tile_pool(name="w", bufs=4))
+        gm_pool = ctx.enter_context(tc.tile_pool(name="gm", bufs=3))
+        dz_pool = ctx.enter_context(tc.tile_pool(name="dz", bufs=2))
+        dzq_pool = ctx.enter_context(tc.tile_pool(name="dzq", bufs=3))
+        gw_pool = ctx.enter_context(tc.tile_pool(name="gw", bufs=2))
+        wq_pool = ctx.enter_context(tc.tile_pool(name="wq", bufs=2))
+        small = ctx.enter_context(tc.tile_pool(name="small", bufs=2))
+        psum_dz = ctx.enter_context(tc.psum_pool(name="psum_dz", bufs=4))
+        psum_w = ctx.enter_context(tc.psum_pool(name="psum_w", bufs=2))
+        psum_acc = ctx.enter_context(tc.psum_pool(name="psum_acc", bufs=2))
+
+        ident = const.tile([P, P], F32)
+        make_identity(nc, ident[:])
+
+        gate_sb = const.tile([P, TOKEN_TILES, 2 * E], F32)
+        g_sb = const.tile([P, TOKEN_TILES, V], BF16)
+        gate_t = const.tile([P, TOKEN_TILES, 2, P, 2], F32)
+
+        def load_zt_half(i, s):
+            rows = zt[i // ROW_TILES, (i % ROW_TILES) * P : (i % ROW_TILES + 1) * P]
+            zt_sb = zt_pool.tile([P, HALF], F32)
+            nc.sync.dma_start(
+                out=zt_sb[:],
+                in_=rows.rearrange("b v e -> b (v e)")[:, s * HALF : (s + 1) * HALF],
+            )
+            return zt_sb
+
+        def load_grad(t):
+            tiles = slice(t * ROW_TILES, (t + 1) * ROW_TILES)
+            nc.sync.dma_start(
+                out=g_sb[:, tiles], in_=grad_out[t].rearrange("(n p) v -> p n v", p=P)
+            )
+
+        def load_w(t, n):
+            w_sb = w_pool.tile([P, K], BF16)
+            nc.sync.dma_start(
+                out=w_sb[:], in_=ew1[t, n * P : (n + 1) * P].rearrange("u v e -> u (v e)")
+            )
+            return w_sb
+
+        def transpose_gates(t):
+            for pair in range(ROW_TILES // 2):
+                bank = psum_w.tile([P, 2, 2 * P], F32, tag="bank")
+                for n in range(2):
+                    i = t * ROW_TILES + 2 * pair + n
+                    spread = small.tile([P, 2, P // 4, 4], F32)
+                    nc.gpsimd.tensor_scalar(
+                        out=spread[:],
+                        in0=gate_sb[:, i, 0:E]
+                        .rearrange("p (j r) -> p r j", r=2)
+                        .unsqueeze(2)
+                        .to_broadcast([P, 2, P // 4, 4]),
+                        scalar1=1.0,
+                        scalar2=0.0,
+                        op0=ALU.mult,
+                        op1=ALU.add,
+                    )
+                    for r in range(2):
+                        nc.tensor.transpose(
+                            bank[:, n, r * P : (r + 1) * P],
+                            spread[:, r].rearrange("p q j -> p (q j)"),
+                            ident[:],
+                        )
+                for n in range(2):
+                    i = t * ROW_TILES + 2 * pair + n
+                    nc.scalar.copy(
+                        out=gate_t[:, i],
+                        in_=bank[:, n]
+                        .rearrange("p (r b) -> p b r", r=2)
+                        .unsqueeze(1)
+                        .to_broadcast([P, 2, P, 2]),
+                    )
+
+        def quantise_w(w_sb, n, wq, ws):
+            gw = gw_pool.tile([P, PASSES, P, 4], BF16, align_bytes=64)
+            gw_words = (
+                gw[:]
+                .rearrange("p c u k -> p (c u k)")
+                .bitcast(F32)
+                .rearrange("p (x h) -> p x h", h=2)
+            )
+            for c0 in range(0, PASSES, 2):
+                bank = psum_w.tile([P, 2, 2 * P], F32, tag="bank")
+                for h in range(2):
+                    for cc in range(2):
+                        first = (c0 + cc) * 2 * P + h * P
+                        nc.tensor.transpose(
+                            bank[:, h, cc * P : (cc + 1) * P],
+                            w_sb[:].bitcast(F32)[:, first : first + P],
+                            ident[:],
+                        )
+                nc.scalar.copy(
+                    out=gw_words[:, c0 * P : (c0 + 2) * P, :],
+                    in_=bank[:].rearrange("p h x -> p x h"),
+                )
+            for c in range(PASSES):
+                nc.vector.quantize_mx(
+                    out=wq[:, c, n * P : (n + 1) * P].bitcast(E4M3X4),
+                    scales=ws[:, c, n * P : (n + 1) * P],
+                    in_=gw[:, c].rearrange("p u k -> p (u k)"),
+                )
+
+        def double_grad(i):
+            g_twice = small.tile([P, V, 2], BF16)
+            nc.gpsimd.tensor_scalar(
+                out=g_twice[:],
+                in0=g_sb[:, i].unsqueeze(2).to_broadcast([P, V, 2]),
+                scalar1=1.0,
+                scalar2=0.0,
+                op0=ALU.mult,
+                op1=ALU.add,
+            )
+            return g_twice
+
+        def mask_grad(gm, s, zt_sb, g_twice):
+            part = gm[:, s * HALF : (s + 1) * HALF]
+            nc.scalar.sign(out=part, in_=zt_sb[:])
+            nc.vector.tensor_scalar_max(out=part, in0=part, scalar1=0.0)
+            nc.vector.tensor_tensor(
+                out=part.rearrange("p (v q r) -> p v q r", q=E // 2, r=2),
+                in0=part.rearrange("p (v q r) -> p v q r", q=E // 2, r=2),
+                in1=g_twice[:, s * (V // 2) : (s + 1) * (V // 2)]
+                .unsqueeze(2)
+                .to_broadcast([P, V // 2, E // 2, 2]),
+                op=ALU.mult,
+            )
+
+        def transpose_gm(gm):
+            banks = []
+            for c0 in range(0, PASSES, 2):
+                bank = psum_dz.tile([P, 2, 2 * P], F32)
+                for h in range(2):
+                    for cc in range(2):
+                        first = (c0 + cc) * 2 * P + h * P
+                        nc.tensor.transpose(
+                            bank[:, h, cc * P : (cc + 1) * P],
+                            gm[:].bitcast(F32)[:, first : first + P],
+                            ident[:],
+                        )
+                banks.append(bank)
+            return banks
+
+        def apply_gates(i, banks):
+            dz = dz_pool.tile([P, PASSES, P, 4], BF16, align_bytes=64)
+            for q in range(PASSES // 2):
+                nc.vector.tensor_tensor(
+                    out=dz[:, 2 * q : 2 * q + 2].rearrange("p c b (h r) -> p (c b) h r", h=2),
+                    in0=banks[q][:]
+                    .rearrange("p h x -> p (h x)")
+                    .bitcast(BF16)
+                    .rearrange("p (h x r) -> p x h r", h=2, r=2),
+                    in1=gate_t[:, i]
+                    .rearrange("p c b r -> p (c b) r")
+                    .unsqueeze(2)
+                    .to_broadcast([P, 2 * P, 2, 2]),
+                    op=ALU.mult,
+                )
+            return dz
+
+        def quantise_dz(dz):
+            dzq = dzq_pool.tile([P, PASSES, P], U32, align_bytes=64)
+            dzs = dzq_pool.tile([P, PASSES, P], U8, align_bytes=64)
+            nc.vector.quantize_mx(
+                out=dzq[:].rearrange("p c b -> p (c b)").bitcast(E5M2X4),
+                scales=dzs[:].rearrange("p c b -> p (c b)"),
+                in_=dz[:].rearrange("p c b k -> p (c b k)"),
+            )
+            return dzq, dzs
+
+        def multiply_and_store(i, dzq, dzs, wq, ws):
+            acc = psum_acc.tile([P, U], F32)
+            for c in range(PASSES):
+                nc.tensor.matmul_mx(
+                    out=acc[:],
+                    lhsT=dzq[:, c, :].bitcast(E5M2X4),
+                    lhsT_scale=dzs[:, c, :],
+                    rhs=wq[:, c, :].bitcast(E4M3X4),
+                    rhs_scale=ws[:, c, :],
+                    start=(c == 0),
+                    stop=(c == PASSES - 1),
+                )
+            res = small.tile([P, U], F32)
+            nc.scalar.copy(out=res[:], in_=acc[:])
+            first = (i % ROW_TILES) * P
+            nc.scalar.dma_start(out=out[i // ROW_TILES, first : first + P, :], in_=res[:])
+
+        def new_w_codes():
+            wq = wq_pool.tile([P, PASSES, U], U32, align_bytes=64)
+            ws = wq_pool.tile([P, PASSES, U], U8, align_bytes=64)
+            return wq, ws
+
+        def masked(i, zt_halves):
+            gm = gm_pool.tile([P, K], BF16)
+            g_twice = double_grad(i)
+            for s in range(2):
+                mask_grad(gm, s, zt_halves[s], g_twice)
+            return gm
+
+        zt_tiles = {0: [load_zt_half(0, 0)]}
+        nc.sync.dma_start(out=gate_sb[:], in_=gate.rearrange("t (n p) e -> p (t n) e", p=P))
+        load_grad(0)
+        zt_tiles[0].append(load_zt_half(0, 1))
+        zt_tiles[1] = [load_zt_half(1, 0), load_zt_half(1, 1)]
+        w_tiles = {(0, n): load_w(0, n) for n in range(ROW_TILES)}
+        zt_tiles[2] = [load_zt_half(2, 0), load_zt_half(2, 1)]
+        load_grad(1)
+
+        w_codes = {0: new_w_codes()}
+        gms = {}
+        banks = {}
+        transpose_gates(0)
+        gms[0] = masked(0, zt_tiles[0])
+        banks[0] = transpose_gm(gms[0])
+        gms[1] = masked(1, zt_tiles[1])
+        for i in range(TOKEN_TILES):
+            if i + 3 < TOKEN_TILES:
+                zt_tiles[i + 3] = [load_zt_half(i + 3, 0), load_zt_half(i + 3, 1)]
+            dz = apply_gates(i, banks[i])
+            if i + 1 < TOKEN_TILES:
+                banks[i + 1] = transpose_gm(gms[i + 1])
+            if i == 0:
+                for n in range(ROW_TILES):
+                    quantise_w(w_tiles[(0, n)], n, w_codes[0][0], w_codes[0][1])
+                w_codes[1] = new_w_codes()
+            if i < ROW_TILES:
+                w_tiles[(1, i)] = load_w(1, i)
+            if i + 2 < TOKEN_TILES:
+                gms[i + 2] = masked(i + 2, zt_tiles[i + 2])
+            dzq, dzs = quantise_dz(dz)
+            wq, ws = w_codes[i // ROW_TILES]
+            multiply_and_store(i, dzq, dzs, wq, ws)
+            if i == 1:
+                transpose_gates(1)
+            if i < ROW_TILES:
+                quantise_w(w_tiles[(1, i)], i, w_codes[1][0], w_codes[1][1])

@@ -177,9 +177,15 @@ def tile_plelayer_pb_v_kernel(
         def apply_gates(i, banks):
             dz = dz_pool.tile([P, PASSES, P, 4], BF16, align_bytes=64)
             for q in range(PASSES // 2):
-                nc.vector.tensor_tensor(
+                if q == 0:
+                    copied = small.tile([P, 2, 2 * P], F32)
+                    nc.scalar.copy(out=copied[:], in_=banks[q][:])
+                    engine, words = nc.gpsimd, copied
+                else:
+                    engine, words = nc.vector, banks[q]
+                engine.tensor_tensor(
                     out=dz[:, 2 * q : 2 * q + 2].rearrange("p c b (h r) -> p (c b) h r", h=2),
-                    in0=banks[q][:]
+                    in0=words[:]
                     .rearrange("p h x -> p (h x)")
                     .bitcast(BF16)
                     .rearrange("p (h x r) -> p x h r", h=2, r=2),

@@ -50,19 +50,22 @@ def tile_plelayer_pb_v_kernel(
         g_sb = const.tile([P, TOKEN_TILES, V], BF16)
         gate_t = const.tile([P, TOKEN_TILES, 2, P, 2], F32)
 
-        def load_zt_half(i, s):
+        def load_zt_half(i, s, pieces):
             rows = zt[i // ROW_TILES, (i % ROW_TILES) * P : (i % ROW_TILES + 1) * P]
+            rows = rows.rearrange("b v e -> b (v e)")
             zt_sb = zt_pool.tile([P, HALF], F32)
-            nc.sync.dma_start(
-                out=zt_sb[:],
-                in_=rows.rearrange("b v e -> b (v e)")[:, s * HALF : (s + 1) * HALF],
-            )
+            width = HALF // pieces
+            for j in range(pieces):
+                nc.sync.dma_start(
+                    out=zt_sb[:, j * width : (j + 1) * width],
+                    in_=rows[:, s * HALF + j * width : s * HALF + (j + 1) * width],
+                )
             return zt_sb
 
-        def load_grad(t):
-            tiles = slice(t * ROW_TILES, (t + 1) * ROW_TILES)
+        def load_grad(first, last):
             nc.sync.dma_start(
-                out=g_sb[:, tiles], in_=grad_out[t].rearrange("(n p) v -> p n v", p=P)
+                out=g_sb[:, first:last],
+                in_=grad_out.rearrange("t (n p) v -> p (t n) v", p=P)[:, first:last],
             )
 
         def load_w(t, n):
@@ -78,16 +81,12 @@ def tile_plelayer_pb_v_kernel(
                 for n in range(2):
                     i = t * ROW_TILES + 2 * pair + n
                     spread = small.tile([P, 2, P // 4, 4], F32)
-                    nc.gpsimd.tensor_scalar(
+                    nc.scalar.copy(
                         out=spread[:],
-                        in0=gate_sb[:, i, 0:E]
+                        in_=gate_sb[:, i, 0:E]
                         .rearrange("p (j r) -> p r j", r=2)
                         .unsqueeze(2)
                         .to_broadcast([P, 2, P // 4, 4]),
-                        scalar1=1.0,
-                        scalar2=0.0,
-                        op0=ALU.mult,
-                        op1=ALU.add,
                     )
                     for r in range(2):
                         nc.tensor.transpose(
@@ -136,28 +135,27 @@ def tile_plelayer_pb_v_kernel(
 
         def double_grad(i):
             g_twice = small.tile([P, V, 2], BF16)
-            nc.gpsimd.tensor_scalar(
-                out=g_twice[:],
-                in0=g_sb[:, i].unsqueeze(2).to_broadcast([P, V, 2]),
-                scalar1=1.0,
-                scalar2=0.0,
-                op0=ALU.mult,
-                op1=ALU.add,
-            )
+            nc.scalar.copy(out=g_twice[:], in_=g_sb[:, i].unsqueeze(2).to_broadcast([P, V, 2]))
             return g_twice
 
-        def mask_grad(gm, s, zt_sb, g_twice):
-            part = gm[:, s * HALF : (s + 1) * HALF]
-            nc.scalar.sign(out=part, in_=zt_sb[:])
-            nc.vector.tensor_scalar_max(out=part, in0=part, scalar1=0.0)
-            nc.vector.tensor_tensor(
-                out=part.rearrange("p (v q r) -> p v q r", q=E // 2, r=2),
-                in0=part.rearrange("p (v q r) -> p v q r", q=E // 2, r=2),
-                in1=g_twice[:, s * (V // 2) : (s + 1) * (V // 2)]
-                .unsqueeze(2)
-                .to_broadcast([P, V // 2, E // 2, 2]),
-                op=ALU.mult,
-            )
+        def masked_by_vector(i, zt_halves):
+            gm = gm_pool.tile([P, K], BF16)
+            for j in range(4):
+                nc.vector.scalar_tensor_tensor(
+                    out=gm[:, j * (K // 4) : (j + 1) * (K // 4)].rearrange(
+                        "p (v e) -> p v e", e=E
+                    ),
+                    in0=zt_halves[j // 2][:, (j % 2) * (K // 4) : (j % 2 + 1) * (K // 4)].rearrange(
+                        "p (v e) -> p v e", e=E
+                    ),
+                    scalar=0.0,
+                    in1=g_sb[:, i, j * (V // 4) : (j + 1) * (V // 4)]
+                    .unsqueeze(2)
+                    .to_broadcast([P, V // 4, E]),
+                    op0=ALU.is_gt,
+                    op1=ALU.mult,
+                )
+            return gm
 
         def transpose_gm(gm):
             banks = []
@@ -174,38 +172,27 @@ def tile_plelayer_pb_v_kernel(
                 banks.append(bank)
             return banks
 
-        def apply_gates(i, banks):
-            dz = dz_pool.tile([P, PASSES, P, 4], BF16, align_bytes=64)
-            for q in range(PASSES // 2):
-                if q == 0:
-                    copied = small.tile([P, 2, 2 * P], F32)
-                    nc.scalar.copy(out=copied[:], in_=banks[q][:])
-                    engine, words = nc.gpsimd, copied
-                else:
-                    engine, words = nc.vector, banks[q]
-                engine.tensor_tensor(
-                    out=dz[:, 2 * q : 2 * q + 2].rearrange("p c b (h r) -> p (c b) h r", h=2),
-                    in0=words[:]
-                    .rearrange("p h x -> p (h x)")
-                    .bitcast(BF16)
-                    .rearrange("p (h x r) -> p x h r", h=2, r=2),
-                    in1=gate_t[:, i]
-                    .rearrange("p c b r -> p (c b) r")
-                    .unsqueeze(2)
-                    .to_broadcast([P, 2 * P, 2, 2]),
-                    op=ALU.mult,
-                )
-            return dz
-
-        def quantise_dz(dz):
-            dzq = dzq_pool.tile([P, PASSES, P], U32, align_bytes=64)
-            dzs = dzq_pool.tile([P, PASSES, P], U8, align_bytes=64)
-            nc.vector.quantize_mx(
-                out=dzq[:].rearrange("p c b -> p (c b)").bitcast(E5M2X4),
-                scales=dzs[:].rearrange("p c b -> p (c b)"),
-                in_=dz[:].rearrange("p c b k -> p (c b k)"),
+        def apply_gates(i, bank, dz, q):
+            nc.vector.tensor_tensor(
+                out=dz[:, 2 * q : 2 * q + 2].rearrange("p c b (h r) -> p (c b) h r", h=2),
+                in0=bank[:]
+                .rearrange("p h x -> p (h x)")
+                .bitcast(BF16)
+                .rearrange("p (h x r) -> p x h r", h=2, r=2),
+                in1=gate_t[:, i]
+                .rearrange("p c b r -> p (c b) r")
+                .unsqueeze(2)
+                .to_broadcast([P, 2 * P, 2, 2]),
+                op=ALU.mult,
             )
-            return dzq, dzs
+
+        def quantise_dz(dz, dzq, dzs, s):
+            passes = slice(s * PASSES // 2, (s + 1) * PASSES // 2)
+            nc.vector.quantize_mx(
+                out=dzq[:, passes].rearrange("p c b -> p (c b)").bitcast(E5M2X4),
+                scales=dzs[:, passes].rearrange("p c b -> p (c b)"),
+                in_=dz[:, passes].rearrange("p c b k -> p (c b k)"),
+            )
 
         def multiply_and_store(i, dzq, dzs, wq, ws):
             acc = psum_acc.tile([P, U], F32)
@@ -232,44 +219,60 @@ def tile_plelayer_pb_v_kernel(
         def masked(i, zt_halves):
             gm = gm_pool.tile([P, K], BF16)
             g_twice = double_grad(i)
+            parts = [gm[:, s * HALF : (s + 1) * HALF] for s in range(2)]
             for s in range(2):
-                mask_grad(gm, s, zt_halves[s], g_twice)
+                nc.scalar.sign(out=parts[s], in_=zt_halves[s][:])
+            for s in range(2):
+                nc.vector.tensor_scalar_max(out=parts[s], in0=parts[s], scalar1=0.0)
+            for s in range(2):
+                nc.vector.tensor_tensor(
+                    out=parts[s].rearrange("p (v q r) -> p v q r", q=E // 2, r=2),
+                    in0=parts[s].rearrange("p (v q r) -> p v q r", q=E // 2, r=2),
+                    in1=g_twice[:, s * (V // 2) : (s + 1) * (V // 2)]
+                    .unsqueeze(2)
+                    .to_broadcast([P, V // 2, E // 2, 2]),
+                    op=ALU.mult,
+                )
             return gm
 
-        zt_tiles = {0: [load_zt_half(0, 0)]}
-        nc.sync.dma_start(out=gate_sb[:], in_=gate.rearrange("t (n p) e -> p (t n) e", p=P))
-        load_grad(0)
-        zt_tiles[0].append(load_zt_half(0, 1))
-        zt_tiles[1] = [load_zt_half(1, 0), load_zt_half(1, 1)]
+        nc.scalar.dma_start(out=gate_sb[:], in_=gate.rearrange("t (n p) e -> p (t n) e", p=P))
+        load_grad(0, 1)
+        zt_tiles = {0: [load_zt_half(0, 0, 2), load_zt_half(0, 1, 2)]}
+        load_grad(1, ROW_TILES)
+        zt_tiles[1] = [load_zt_half(1, 0, 1), load_zt_half(1, 1, 1)]
         w_tiles = {(0, n): load_w(0, n) for n in range(ROW_TILES)}
-        zt_tiles[2] = [load_zt_half(2, 0), load_zt_half(2, 1)]
-        load_grad(1)
+        zt_tiles[2] = [load_zt_half(2, 0, 1), load_zt_half(2, 1, 1)]
+        load_grad(ROW_TILES, TOKEN_TILES)
 
         w_codes = {0: new_w_codes()}
         gms = {}
         banks = {}
         transpose_gates(0)
-        gms[0] = masked(0, zt_tiles[0])
+        gms[0] = masked_by_vector(0, zt_tiles[0])
         banks[0] = transpose_gm(gms[0])
         gms[1] = masked(1, zt_tiles[1])
         for i in range(TOKEN_TILES):
             if i + 3 < TOKEN_TILES:
-                zt_tiles[i + 3] = [load_zt_half(i + 3, 0), load_zt_half(i + 3, 1)]
-            dz = apply_gates(i, banks[i])
+                zt_tiles[i + 3] = [load_zt_half(i + 3, 0, 1), load_zt_half(i + 3, 1, 1)]
+            dz = dz_pool.tile([P, PASSES, P, 4], BF16, align_bytes=64)
+            dzq = dzq_pool.tile([P, PASSES, P], U32, align_bytes=64)
+            dzs = dzq_pool.tile([P, PASSES, P], U8, align_bytes=64)
+            for q in range(PASSES // 2):
+                apply_gates(i, banks[i][q], dz, q)
             if i + 1 < TOKEN_TILES:
                 banks[i + 1] = transpose_gm(gms[i + 1])
             if i == 0:
                 for n in range(ROW_TILES):
-                    quantise_w(w_tiles[(0, n)], n, w_codes[0][0], w_codes[0][1])
+                    quantise_w(w_tiles[(0, n)], n, *w_codes[0])
                 w_codes[1] = new_w_codes()
             if i < ROW_TILES:
                 w_tiles[(1, i)] = load_w(1, i)
             if i + 2 < TOKEN_TILES:
                 gms[i + 2] = masked(i + 2, zt_tiles[i + 2])
-            dzq, dzs = quantise_dz(dz)
-            wq, ws = w_codes[i // ROW_TILES]
-            multiply_and_store(i, dzq, dzs, wq, ws)
+            for s in range(2):
+                quantise_dz(dz, dzq, dzs, s)
+            multiply_and_store(i, dzq, dzs, *w_codes[i // ROW_TILES])
             if i == 1:
                 transpose_gates(1)
             if i < ROW_TILES:
-                quantise_w(w_tiles[(1, i)], i, w_codes[1][0], w_codes[1][1])
+                quantise_w(w_tiles[(1, i)], i, *w_codes[1])

@@ -133,11 +133,6 @@ def tile_plelayer_pb_v_kernel(
                     in_=gw[:, c].rearrange("p u k -> p (u k)"),
                 )
 
-        def double_grad(i):
-            g_twice = small.tile([P, V, 2], BF16)
-            nc.scalar.copy(out=g_twice[:], in_=g_sb[:, i].unsqueeze(2).to_broadcast([P, V, 2]))
-            return g_twice
-
         def masked_by_vector(i, zt_halves):
             gm = gm_pool.tile([P, K], BF16)
             for j in range(4):
@@ -216,25 +211,6 @@ def tile_plelayer_pb_v_kernel(
             ws = wq_pool.tile([P, PASSES, U], U8, align_bytes=64)
             return wq, ws
 
-        def masked(i, zt_halves):
-            gm = gm_pool.tile([P, K], BF16)
-            g_twice = double_grad(i)
-            parts = [gm[:, s * HALF : (s + 1) * HALF] for s in range(2)]
-            for s in range(2):
-                nc.scalar.sign(out=parts[s], in_=zt_halves[s][:])
-            for s in range(2):
-                nc.vector.tensor_scalar_max(out=parts[s], in0=parts[s], scalar1=0.0)
-            for s in range(2):
-                nc.vector.tensor_tensor(
-                    out=parts[s].rearrange("p (v q r) -> p v q r", q=E // 2, r=2),
-                    in0=parts[s].rearrange("p (v q r) -> p v q r", q=E // 2, r=2),
-                    in1=g_twice[:, s * (V // 2) : (s + 1) * (V // 2)]
-                    .unsqueeze(2)
-                    .to_broadcast([P, V // 2, E // 2, 2]),
-                    op=ALU.mult,
-                )
-            return gm
-
         nc.scalar.dma_start(out=gate_sb[:], in_=gate.rearrange("t (n p) e -> p (t n) e", p=P))
         load_grad(0, 1)
         zt_tiles = {0: [load_zt_half(0, 0, 2), load_zt_half(0, 1, 2)]}
@@ -250,7 +226,7 @@ def tile_plelayer_pb_v_kernel(
         transpose_gates(0)
         gms[0] = masked_by_vector(0, zt_tiles[0])
         banks[0] = transpose_gm(gms[0])
-        gms[1] = masked(1, zt_tiles[1])
+        gms[1] = masked_by_vector(1, zt_tiles[1])
         for i in range(TOKEN_TILES):
             if i + 3 < TOKEN_TILES:
                 zt_tiles[i + 3] = [load_zt_half(i + 3, 0, 1), load_zt_half(i + 3, 1, 1)]
@@ -268,7 +244,7 @@ def tile_plelayer_pb_v_kernel(
             if i < ROW_TILES:
                 w_tiles[(1, i)] = load_w(1, i)
             if i + 2 < TOKEN_TILES:
-                gms[i + 2] = masked(i + 2, zt_tiles[i + 2])
+                gms[i + 2] = masked_by_vector(i + 2, zt_tiles[i + 2])
             for s in range(2):
                 quantise_dz(dz, dzq, dzs, s)
             multiply_and_store(i, dzq, dzs, *w_codes[i // ROW_TILES])

@@ -18,8 +18,8 @@ K_PASS = 4 * P
 PASSES = K // K_PASS
 ROW_TILES = B // P
 TOKEN_TILES = T * ROW_TILES
-WORDS = K // 2
 HALF = K // 2
+QUARTER = K // 4
 
 FLOPS = 2 * T * B * U * K
 BYTES = 4 * T * B * K + 2 * T * U * K + 2 * T * B * V + 4 * T * B * E + 4 * T * B * U
@@ -32,8 +32,8 @@ def tile_plelayer_pb_v_kernel(
     with ExitStack() as ctx:
         const = ctx.enter_context(tc.tile_pool(name="const", bufs=1))
         zt_pool = ctx.enter_context(tc.tile_pool(name="zt", bufs=6))
-        w_pool = ctx.enter_context(tc.tile_pool(name="w", bufs=4))
-        gm_pool = ctx.enter_context(tc.tile_pool(name="gm", bufs=3))
+        w_pool = ctx.enter_context(tc.tile_pool(name="w", bufs=3))
+        gm_pool = ctx.enter_context(tc.tile_pool(name="gm", bufs=4))
         dz_pool = ctx.enter_context(tc.tile_pool(name="dz", bufs=2))
         dzq_pool = ctx.enter_context(tc.tile_pool(name="dzq", bufs=3))
         gw_pool = ctx.enter_context(tc.tile_pool(name="gw", bufs=2))
@@ -75,11 +75,17 @@ def tile_plelayer_pb_v_kernel(
             )
             return w_sb
 
+        def transpose_block(bank, h, cc, row_words, c):
+            first = c * 2 * P + h * P
+            nc.tensor.transpose(
+                bank[:, h, cc * P : (cc + 1) * P], row_words[:, first : first + P], ident[:]
+            )
+
         def transpose_gates(t):
             for pair in range(ROW_TILES // 2):
                 bank = psum_w.tile([P, 2, 2 * P], F32, tag="bank")
-                for n in range(2):
-                    i = t * ROW_TILES + 2 * pair + n
+                for m in range(2):
+                    i = t * ROW_TILES + 2 * pair + m
                     spread = small.tile([P, 2, P // 4, 4], F32)
                     nc.scalar.copy(
                         out=spread[:],
@@ -90,15 +96,15 @@ def tile_plelayer_pb_v_kernel(
                     )
                     for r in range(2):
                         nc.tensor.transpose(
-                            bank[:, n, r * P : (r + 1) * P],
-                            spread[:, r].rearrange("p q j -> p (q j)"),
+                            bank[:, m, r * P : (r + 1) * P],
+                            spread[:, r].rearrange("p a j -> p (a j)"),
                             ident[:],
                         )
-                for n in range(2):
-                    i = t * ROW_TILES + 2 * pair + n
+                for m in range(2):
+                    i = t * ROW_TILES + 2 * pair + m
                     nc.scalar.copy(
                         out=gate_t[:, i],
-                        in_=bank[:, n]
+                        in_=bank[:, m]
                         .rearrange("p (r b) -> p b r", r=2)
                         .unsqueeze(1)
                         .to_broadcast([P, 2, P, 2]),
@@ -116,12 +122,7 @@ def tile_plelayer_pb_v_kernel(
                 bank = psum_w.tile([P, 2, 2 * P], F32, tag="bank")
                 for h in range(2):
                     for cc in range(2):
-                        first = (c0 + cc) * 2 * P + h * P
-                        nc.tensor.transpose(
-                            bank[:, h, cc * P : (cc + 1) * P],
-                            w_sb[:].bitcast(F32)[:, first : first + P],
-                            ident[:],
-                        )
+                        transpose_block(bank, h, cc, w_sb[:].bitcast(F32), c0 + cc)
                 nc.scalar.copy(
                     out=gw_words[:, c0 * P : (c0 + 2) * P, :],
                     in_=bank[:].rearrange("p h x -> p x h"),
@@ -133,16 +134,18 @@ def tile_plelayer_pb_v_kernel(
                     in_=gw[:, c].rearrange("p u k -> p (u k)"),
                 )
 
+        def double_grad(i):
+            g_twice = small.tile([P, V, 2], BF16)
+            nc.scalar.copy(out=g_twice[:], in_=g_sb[:, i].unsqueeze(2).to_broadcast([P, V, 2]))
+            return g_twice
+
         def masked_by_vector(i, zt_halves):
             gm = gm_pool.tile([P, K], BF16)
-            for j in range(4):
+            for j in range(K // QUARTER):
+                zt_quarter = zt_halves[j // 2][:, (j % 2) * QUARTER : (j % 2 + 1) * QUARTER]
                 nc.vector.scalar_tensor_tensor(
-                    out=gm[:, j * (K // 4) : (j + 1) * (K // 4)].rearrange(
-                        "p (v e) -> p v e", e=E
-                    ),
-                    in0=zt_halves[j // 2][:, (j % 2) * (K // 4) : (j % 2 + 1) * (K // 4)].rearrange(
-                        "p (v e) -> p v e", e=E
-                    ),
+                    out=gm[:, j * QUARTER : (j + 1) * QUARTER].rearrange("p (v e) -> p v e", e=E),
+                    in0=zt_quarter.rearrange("p (v e) -> p v e", e=E),
                     scalar=0.0,
                     in1=g_sb[:, i, j * (V // 4) : (j + 1) * (V // 4)]
                     .unsqueeze(2)
@@ -152,18 +155,32 @@ def tile_plelayer_pb_v_kernel(
                 )
             return gm
 
+        def masked(i, zt_halves):
+            gm = gm_pool.tile([P, K], BF16)
+            g_twice = double_grad(i)
+            parts = [gm[:, s * HALF : (s + 1) * HALF] for s in range(2)]
+            for s in range(2):
+                nc.scalar.sign(out=parts[s], in_=zt_halves[s][:])
+            for s in range(2):
+                nc.vector.tensor_scalar_max(out=parts[s], in0=parts[s], scalar1=0.0)
+            for s in range(2):
+                nc.vector.tensor_tensor(
+                    out=parts[s].rearrange("p (v a r) -> p v a r", a=E // 2, r=2),
+                    in0=parts[s].rearrange("p (v a r) -> p v a r", a=E // 2, r=2),
+                    in1=g_twice[:, s * (V // 2) : (s + 1) * (V // 2)]
+                    .unsqueeze(2)
+                    .to_broadcast([P, V // 2, E // 2, 2]),
+                    op=ALU.mult,
+                )
+            return gm
+
         def transpose_gm(gm):
             banks = []
             for c0 in range(0, PASSES, 2):
                 bank = psum_dz.tile([P, 2, 2 * P], F32)
                 for h in range(2):
                     for cc in range(2):
-                        first = (c0 + cc) * 2 * P + h * P
-                        nc.tensor.transpose(
-                            bank[:, h, cc * P : (cc + 1) * P],
-                            gm[:].bitcast(F32)[:, first : first + P],
-                            ident[:],
-                        )
+                        transpose_block(bank, h, cc, gm[:].bitcast(F32), c0 + cc)
                 banks.append(bank)
             return banks
 
@@ -181,8 +198,8 @@ def tile_plelayer_pb_v_kernel(
                 op=ALU.mult,
             )
 
-        def quantise_dz(dz, dzq, dzs, s):
-            passes = slice(s * PASSES // 2, (s + 1) * PASSES // 2)
+        def quantise_dz(dz, dzq, dzs, q):
+            passes = slice(2 * q, 2 * q + 2)
             nc.vector.quantize_mx(
                 out=dzq[:, passes].rearrange("p c b -> p (c b)").bitcast(E5M2X4),
                 scales=dzs[:, passes].rearrange("p c b -> p (c b)"),
@@ -226,7 +243,7 @@ def tile_plelayer_pb_v_kernel(
         transpose_gates(0)
         gms[0] = masked_by_vector(0, zt_tiles[0])
         banks[0] = transpose_gm(gms[0])
-        gms[1] = masked_by_vector(1, zt_tiles[1])
+        gms[1] = masked(1, zt_tiles[1])
         for i in range(TOKEN_TILES):
             if i + 3 < TOKEN_TILES:
                 zt_tiles[i + 3] = [load_zt_half(i + 3, 0, 1), load_zt_half(i + 3, 1, 1)]
@@ -244,9 +261,9 @@ def tile_plelayer_pb_v_kernel(
             if i < ROW_TILES:
                 w_tiles[(1, i)] = load_w(1, i)
             if i + 2 < TOKEN_TILES:
-                gms[i + 2] = masked_by_vector(i + 2, zt_tiles[i + 2])
-            for s in range(2):
-                quantise_dz(dz, dzq, dzs, s)
+                gms[i + 2] = masked(i + 2, zt_tiles[i + 2])
+            for q in range(PASSES // 2):
+                quantise_dz(dz, dzq, dzs, q)
             multiply_and_store(i, dzq, dzs, *w_codes[i // ROW_TILES])
             if i == 1:
                 transpose_gates(1)

@@ -10,6 +10,7 @@ U8 = mybir.dt.uint8
 E4M3X4 = mybir.dt.float8_e4m3fn_x4
 E5M2X4 = mybir.dt.float8_e5m2_x4
 ALU = mybir.AluOpType
+COPY = mybir.ActivationFunctionType.Copy
 
 P = 128
 T, B, U, V, E = 2, 512, 512, 512, 8
@@ -19,7 +20,7 @@ PASSES = K // K_PASS
 ROW_TILES = B // P
 TOKEN_TILES = T * ROW_TILES
 HALF = K // 2
-QUARTER = K // 4
+SCALAR_EXPERTS = (0, 4, 4, 4, 4, 4, 4, 4)
 
 FLOPS = 2 * T * B * U * K
 BYTES = 4 * T * B * K + 2 * T * U * K + 2 * T * B * V + 4 * T * B * E + 4 * T * B * U
@@ -33,7 +34,8 @@ def tile_plelayer_pb_v_kernel(
         const = ctx.enter_context(tc.tile_pool(name="const", bufs=1))
         zt_pool = ctx.enter_context(tc.tile_pool(name="zt", bufs=6))
         w_pool = ctx.enter_context(tc.tile_pool(name="w", bufs=3))
-        gm_pool = ctx.enter_context(tc.tile_pool(name="gm", bufs=4))
+        y_pool = ctx.enter_context(tc.tile_pool(name="y", bufs=2))
+        rows_pool = ctx.enter_context(tc.tile_pool(name="rows", bufs=3))
         dz_pool = ctx.enter_context(tc.tile_pool(name="dz", bufs=2))
         dzq_pool = ctx.enter_context(tc.tile_pool(name="dzq", bufs=3))
         gw_pool = ctx.enter_context(tc.tile_pool(name="gw", bufs=2))
@@ -48,7 +50,6 @@ def tile_plelayer_pb_v_kernel(
 
         gate_sb = const.tile([P, TOKEN_TILES, 2 * E], F32)
         g_sb = const.tile([P, TOKEN_TILES, V], BF16)
-        gate_t = const.tile([P, TOKEN_TILES, 2, P, 2], F32)
 
         def load_zt_half(i, s, pieces):
             rows = zt[i // ROW_TILES, (i % ROW_TILES) * P : (i % ROW_TILES + 1) * P]
@@ -75,128 +76,88 @@ def tile_plelayer_pb_v_kernel(
             )
             return w_sb
 
-        def transpose_block(bank, h, cc, row_words, c):
-            first = c * 2 * P + h * P
-            nc.tensor.transpose(
-                bank[:, h, cc * P : (cc + 1) * P], row_words[:, first : first + P], ident[:]
-            )
-
-        def transpose_gates(t):
-            for pair in range(ROW_TILES // 2):
-                bank = psum_w.tile([P, 2, 2 * P], F32, tag="bank")
-                for m in range(2):
-                    i = t * ROW_TILES + 2 * pair + m
-                    spread = small.tile([P, 2, P // 4, 4], F32)
-                    nc.scalar.copy(
-                        out=spread[:],
-                        in_=gate_sb[:, i, 0:E]
-                        .rearrange("p (j r) -> p r j", r=2)
-                        .unsqueeze(2)
-                        .to_broadcast([P, 2, P // 4, 4]),
-                    )
-                    for r in range(2):
-                        nc.tensor.transpose(
-                            bank[:, m, r * P : (r + 1) * P],
-                            spread[:, r].rearrange("p a j -> p (a j)"),
-                            ident[:],
+        def grad_times_gate(i):
+            y = y_pool.tile([P, 2, 4, V], BF16)
+            for u in range(2):
+                for q in range(4):
+                    e = 4 * (q // 2) + 2 * u + q % 2
+                    if u == 1 and q < SCALAR_EXPERTS[i]:
+                        nc.scalar.activation(
+                            out=y[:, u, q, :], in_=g_sb[:, i], func=COPY, scale=gate_sb[:, i, e : e + 1]
                         )
-                for m in range(2):
-                    i = t * ROW_TILES + 2 * pair + m
-                    nc.scalar.copy(
-                        out=gate_t[:, i],
-                        in_=bank[:, m]
-                        .rearrange("p (r b) -> p b r", r=2)
-                        .unsqueeze(1)
-                        .to_broadcast([P, 2, P, 2]),
-                    )
+                    else:
+                        nc.vector.tensor_scalar_mul(
+                            out=y[:, u, q, :], in0=g_sb[:, i], scalar1=gate_sb[:, i, e : e + 1]
+                        )
+            return y
 
-        def quantise_w(w_sb, n, wq, ws):
-            gw = gw_pool.tile([P, PASSES, P, 4], BF16, align_bytes=64)
-            gw_words = (
-                gw[:]
-                .rearrange("p c u k -> p (c u k)")
+        def masked_rows(y, zt_halves, pieces):
+            rows = rows_pool.tile([P, 2, V, 2, 2], BF16)
+            nv = V // 2 // pieces
+            for s in range(2):
+                for j in range(pieces):
+                    for u in range(2):
+                        v0 = s * (V // 2) + j * nv
+                        nc.vector.scalar_tensor_tensor(
+                            out=rows[:, u, v0 : v0 + nv],
+                            in0=zt_halves[s][:, j * nv * E : (j + 1) * nv * E].rearrange(
+                                "p (v a j r) -> p v a j r", a=2, j=2, r=2
+                            )[:, :, :, u, :],
+                            scalar=0.0,
+                            in1=y[:, u, :, v0 : v0 + nv].rearrange("p (a r) v -> p v a r", a=2),
+                            op0=ALU.is_gt,
+                            op1=ALU.mult,
+                        )
+            return rows
+
+        def copy_out(bank, packed, c0):
+            words = (
+                packed[:]
+                .rearrange("p c x k -> p (c x k)")
                 .bitcast(F32)
-                .rearrange("p (x h) -> p x h", h=2)
+                .rearrange("p (x u) -> p x u", u=2)
             )
+            nc.scalar.copy(
+                out=words[:, c0 * P : (c0 + 2) * P, :], in_=bank[:].rearrange("p u x -> p x u")
+            )
+
+        def to_k_major(rows):
+            words = rows[:].rearrange("p u v a r -> p (u v a r)").bitcast(F32)
+            dz = dz_pool.tile([P, PASSES, P, 4], BF16, align_bytes=64)
+            for c0 in range(0, PASSES, 2):
+                bank = psum_dz.tile([P, 2, 2 * P], F32)
+                for u in range(2):
+                    for cc in range(2):
+                        first = u * (K // 4) + (c0 + cc) * P
+                        nc.tensor.transpose(
+                            bank[:, u, cc * P : (cc + 1) * P], words[:, first : first + P], ident[:]
+                        )
+                copy_out(bank, dz, c0)
+            return dz
+
+        def transpose_w(w_sb):
+            words = w_sb[:].bitcast(F32)
+            gw = gw_pool.tile([P, PASSES, P, 4], BF16, align_bytes=64)
             for c0 in range(0, PASSES, 2):
                 bank = psum_w.tile([P, 2, 2 * P], F32, tag="bank")
-                for h in range(2):
+                for u in range(2):
                     for cc in range(2):
-                        transpose_block(bank, h, cc, w_sb[:].bitcast(F32), c0 + cc)
-                nc.scalar.copy(
-                    out=gw_words[:, c0 * P : (c0 + 2) * P, :],
-                    in_=bank[:].rearrange("p h x -> p x h"),
-                )
+                        first = (c0 + cc) * 2 * P
+                        nc.tensor.transpose(
+                            bank[:, u, cc * P : (cc + 1) * P],
+                            words[:, first + u : first + 2 * P : 2],
+                            ident[:],
+                        )
+                copy_out(bank, gw, c0)
+            return gw
+
+        def quantise_w(gw, n, wq, ws):
             for c in range(PASSES):
                 nc.vector.quantize_mx(
                     out=wq[:, c, n * P : (n + 1) * P].bitcast(E4M3X4),
                     scales=ws[:, c, n * P : (n + 1) * P],
                     in_=gw[:, c].rearrange("p u k -> p (u k)"),
                 )
-
-        def double_grad(i):
-            g_twice = small.tile([P, V, 2], BF16)
-            nc.scalar.copy(out=g_twice[:], in_=g_sb[:, i].unsqueeze(2).to_broadcast([P, V, 2]))
-            return g_twice
-
-        def masked_by_vector(i, zt_halves):
-            gm = gm_pool.tile([P, K], BF16)
-            for j in range(K // QUARTER):
-                zt_quarter = zt_halves[j // 2][:, (j % 2) * QUARTER : (j % 2 + 1) * QUARTER]
-                nc.vector.scalar_tensor_tensor(
-                    out=gm[:, j * QUARTER : (j + 1) * QUARTER].rearrange("p (v e) -> p v e", e=E),
-                    in0=zt_quarter.rearrange("p (v e) -> p v e", e=E),
-                    scalar=0.0,
-                    in1=g_sb[:, i, j * (V // 4) : (j + 1) * (V // 4)]
-                    .unsqueeze(2)
-                    .to_broadcast([P, V // 4, E]),
-                    op0=ALU.is_gt,
-                    op1=ALU.mult,
-                )
-            return gm
-
-        def masked(i, zt_halves):
-            gm = gm_pool.tile([P, K], BF16)
-            g_twice = double_grad(i)
-            parts = [gm[:, s * HALF : (s + 1) * HALF] for s in range(2)]
-            for s in range(2):
-                nc.scalar.sign(out=parts[s], in_=zt_halves[s][:])
-            for s in range(2):
-                nc.vector.tensor_scalar_max(out=parts[s], in0=parts[s], scalar1=0.0)
-            for s in range(2):
-                nc.vector.tensor_tensor(
-                    out=parts[s].rearrange("p (v a r) -> p v a r", a=E // 2, r=2),
-                    in0=parts[s].rearrange("p (v a r) -> p v a r", a=E // 2, r=2),
-                    in1=g_twice[:, s * (V // 2) : (s + 1) * (V // 2)]
-                    .unsqueeze(2)
-                    .to_broadcast([P, V // 2, E // 2, 2]),
-                    op=ALU.mult,
-                )
-            return gm
-
-        def transpose_gm(gm):
-            banks = []
-            for c0 in range(0, PASSES, 2):
-                bank = psum_dz.tile([P, 2, 2 * P], F32)
-                for h in range(2):
-                    for cc in range(2):
-                        transpose_block(bank, h, cc, gm[:].bitcast(F32), c0 + cc)
-                banks.append(bank)
-            return banks
-
-        def apply_gates(i, bank, dz, q):
-            nc.vector.tensor_tensor(
-                out=dz[:, 2 * q : 2 * q + 2].rearrange("p c b (h r) -> p (c b) h r", h=2),
-                in0=bank[:]
-                .rearrange("p h x -> p (h x)")
-                .bitcast(BF16)
-                .rearrange("p (h x r) -> p x h r", h=2, r=2),
-                in1=gate_t[:, i]
-                .rearrange("p c b r -> p (c b) r")
-                .unsqueeze(2)
-                .to_broadcast([P, 2 * P, 2, 2]),
-                op=ALU.mult,
-            )
 
         def quantise_dz(dz, dzq, dzs, q):
             passes = slice(2 * q, 2 * q + 2)
@@ -238,34 +199,26 @@ def tile_plelayer_pb_v_kernel(
         load_grad(ROW_TILES, TOKEN_TILES)
 
         w_codes = {0: new_w_codes()}
-        gms = {}
-        banks = {}
-        transpose_gates(0)
-        gms[0] = masked_by_vector(0, zt_tiles[0])
-        banks[0] = transpose_gm(gms[0])
-        gms[1] = masked(1, zt_tiles[1])
+        ys = {0: grad_times_gate(0)}
+        dzs_k = {0: to_k_major(masked_rows(ys[0], zt_tiles[0], 2))}
+        ys[1] = grad_times_gate(1)
         for i in range(TOKEN_TILES):
             if i + 3 < TOKEN_TILES:
                 zt_tiles[i + 3] = [load_zt_half(i + 3, 0, 1), load_zt_half(i + 3, 1, 1)]
-            dz = dz_pool.tile([P, PASSES, P, 4], BF16, align_bytes=64)
+            if i < ROW_TILES:
+                w_tiles[(1, i)] = load_w(1, i)
+            if i + 1 < TOKEN_TILES:
+                dzs_k[i + 1] = to_k_major(masked_rows(ys[i + 1], zt_tiles[i + 1], 1))
+            if i + 2 < TOKEN_TILES:
+                ys[i + 2] = grad_times_gate(i + 2)
+            if i == 0:
+                for n in range(ROW_TILES):
+                    quantise_w(transpose_w(w_tiles[(0, n)]), n, *w_codes[0])
+                w_codes[1] = new_w_codes()
             dzq = dzq_pool.tile([P, PASSES, P], U32, align_bytes=64)
             dzs = dzq_pool.tile([P, PASSES, P], U8, align_bytes=64)
             for q in range(PASSES // 2):
-                apply_gates(i, banks[i][q], dz, q)
-            if i + 1 < TOKEN_TILES:
-                banks[i + 1] = transpose_gm(gms[i + 1])
-            if i == 0:
-                for n in range(ROW_TILES):
-                    quantise_w(w_tiles[(0, n)], n, *w_codes[0])
-                w_codes[1] = new_w_codes()
-            if i < ROW_TILES:
-                w_tiles[(1, i)] = load_w(1, i)
-            if i + 2 < TOKEN_TILES:
-                gms[i + 2] = masked(i + 2, zt_tiles[i + 2])
-            for q in range(PASSES // 2):
-                quantise_dz(dz, dzq, dzs, q)
+                quantise_dz(dzs_k[i], dzq, dzs, q)
             multiply_and_store(i, dzq, dzs, *w_codes[i // ROW_TILES])
-            if i == 1:
-                transpose_gates(1)
             if i < ROW_TILES:
-                quantise_w(w_tiles[(1, i)], i, *w_codes[1])
+                quantise_w(transpose_w(w_tiles[(1, i)]), i, *w_codes[1])

@@ -20,6 +20,7 @@ PASSES = K // K_PASS
 ROW_TILES = B // P
 TOKEN_TILES = T * ROW_TILES
 HALF = K // 2
+HALF_THROUGH_PSUM = (2, 3, 4, 5, 6, 7)
 SCALAR_EXPERTS = (0, 4, 4, 4, 4, 4, 4, 4)
 
 FLOPS = 2 * T * B * U * K
@@ -34,19 +35,22 @@ def tile_plelayer_pb_v_kernel(
         const = ctx.enter_context(tc.tile_pool(name="const", bufs=1))
         zt_pool = ctx.enter_context(tc.tile_pool(name="zt", bufs=6))
         w_pool = ctx.enter_context(tc.tile_pool(name="w", bufs=3))
-        y_pool = ctx.enter_context(tc.tile_pool(name="y", bufs=2))
+        y_pool = ctx.enter_context(tc.tile_pool(name="y", bufs=3))
         rows_pool = ctx.enter_context(tc.tile_pool(name="rows", bufs=3))
-        dz_pool = ctx.enter_context(tc.tile_pool(name="dz", bufs=2))
-        dzq_pool = ctx.enter_context(tc.tile_pool(name="dzq", bufs=3))
+        dz_pool = ctx.enter_context(tc.tile_pool(name="dz", bufs=3))
+        dzq_pool = ctx.enter_context(tc.tile_pool(name="dzq", bufs=4))
         gw_pool = ctx.enter_context(tc.tile_pool(name="gw", bufs=2))
         wq_pool = ctx.enter_context(tc.tile_pool(name="wq", bufs=2))
         small = ctx.enter_context(tc.tile_pool(name="small", bufs=2))
-        psum_dz = ctx.enter_context(tc.psum_pool(name="psum_dz", bufs=4))
+        psum_dz = ctx.enter_context(tc.psum_pool(name="psum_dz", bufs=2))
+        psum_y = ctx.enter_context(tc.psum_pool(name="psum_y", bufs=2))
         psum_w = ctx.enter_context(tc.psum_pool(name="psum_w", bufs=2))
         psum_acc = ctx.enter_context(tc.psum_pool(name="psum_acc", bufs=2))
 
         ident = const.tile([P, P], F32)
         make_identity(nc, ident[:])
+        ident_bf = const.tile([P, P], BF16)
+        make_identity(nc, ident_bf[:])
 
         gate_sb = const.tile([P, TOKEN_TILES, 2 * E], F32)
         g_sb = const.tile([P, TOKEN_TILES, V], BF16)
@@ -91,23 +95,42 @@ def tile_plelayer_pb_v_kernel(
                         )
             return y
 
-        def masked_rows(y, zt_halves, pieces):
+        def y_in_psum(y, u):
+            nv = V // 2
+            bank = psum_y.tile([P, 4, nv], BF16)
+            for m in range(2):
+                nc.tensor.matmul(
+                    out=bank[:, 2 * m : 2 * m + 2, :],
+                    lhsT=ident_bf[:],
+                    rhs=y[:, u, 2 * m : 2 * m + 2, 0:nv],
+                    start=True,
+                    stop=True,
+                )
+            return bank
+
+        def masked_rows(y, zt_halves, pieces, banks, after_first_half):
             rows = rows_pool.tile([P, 2, V, 2, 2], BF16)
             nv = V // 2 // pieces
             for s in range(2):
                 for j in range(pieces):
                     for u in range(2):
                         v0 = s * (V // 2) + j * nv
+                        if s == 0 and banks:
+                            y_part = banks[u][:]
+                        else:
+                            y_part = y[:, u, :, v0 : v0 + nv]
                         nc.vector.scalar_tensor_tensor(
                             out=rows[:, u, v0 : v0 + nv],
                             in0=zt_halves[s][:, j * nv * E : (j + 1) * nv * E].rearrange(
                                 "p (v a j r) -> p v a j r", a=2, j=2, r=2
                             )[:, :, :, u, :],
                             scalar=0.0,
-                            in1=y[:, u, :, v0 : v0 + nv].rearrange("p (a r) v -> p v a r", a=2),
+                            in1=y_part.rearrange("p (a r) v -> p v a r", a=2),
                             op0=ALU.is_gt,
                             op1=ALU.mult,
                         )
+                if s == 0:
+                    after_first_half()
             return rows
 
         def copy_out(bank, packed, c0):
@@ -200,17 +223,27 @@ def tile_plelayer_pb_v_kernel(
 
         w_codes = {0: new_w_codes()}
         ys = {0: grad_times_gate(0)}
-        dzs_k = {0: to_k_major(masked_rows(ys[0], zt_tiles[0], 2))}
+        dzs_k = {0: to_k_major(masked_rows(ys[0], zt_tiles[0], 2, [], lambda: None))}
         ys[1] = grad_times_gate(1)
+        copies = {}
+
+        def copy_next(n):
+            if n in HALF_THROUGH_PSUM:
+                copies[n] = [y_in_psum(ys[n], u) for u in range(2)]
+
         for i in range(TOKEN_TILES):
-            if i + 3 < TOKEN_TILES:
-                zt_tiles[i + 3] = [load_zt_half(i + 3, 0, 1), load_zt_half(i + 3, 1, 1)]
             if i < ROW_TILES:
                 w_tiles[(1, i)] = load_w(1, i)
-            if i + 1 < TOKEN_TILES:
-                dzs_k[i + 1] = to_k_major(masked_rows(ys[i + 1], zt_tiles[i + 1], 1))
+            if i + 3 < TOKEN_TILES:
+                zt_tiles[i + 3] = [load_zt_half(i + 3, 0, 1), load_zt_half(i + 3, 1, 1)]
             if i + 2 < TOKEN_TILES:
                 ys[i + 2] = grad_times_gate(i + 2)
+            if i + 1 < TOKEN_TILES:
+                dzs_k[i + 1] = to_k_major(
+                    masked_rows(
+                        ys[i + 1], zt_tiles[i + 1], 1, copies.get(i + 1, []), lambda: copy_next(i + 2)
+                    )
+                )
             if i == 0:
                 for n in range(ROW_TILES):
                     quantise_w(transpose_w(w_tiles[(0, n)]), n, *w_codes[0])

@@ -42,9 +42,8 @@ def tile_plelayer_pb_v_kernel(
         gw_pool = ctx.enter_context(tc.tile_pool(name="gw", bufs=2))
         wq_pool = ctx.enter_context(tc.tile_pool(name="wq", bufs=2))
         small = ctx.enter_context(tc.tile_pool(name="small", bufs=2))
-        psum_dz = ctx.enter_context(tc.psum_pool(name="psum_dz", bufs=2))
+        psum_t = ctx.enter_context(tc.psum_pool(name="psum_t", bufs=4))
         psum_y = ctx.enter_context(tc.psum_pool(name="psum_y", bufs=2))
-        psum_w = ctx.enter_context(tc.psum_pool(name="psum_w", bufs=2))
         psum_acc = ctx.enter_context(tc.psum_pool(name="psum_acc", bufs=2))
 
         ident = const.tile([P, P], F32)
@@ -148,7 +147,7 @@ def tile_plelayer_pb_v_kernel(
             words = rows[:].rearrange("p u v a r -> p (u v a r)").bitcast(F32)
             dz = dz_pool.tile([P, PASSES, P, 4], BF16, align_bytes=64)
             for c0 in range(0, PASSES, 2):
-                bank = psum_dz.tile([P, 2, 2 * P], F32)
+                bank = psum_t.tile([P, 2, 2 * P], F32, tag="bank")
                 for u in range(2):
                     for cc in range(2):
                         first = u * (K // 4) + (c0 + cc) * P
@@ -162,7 +161,7 @@ def tile_plelayer_pb_v_kernel(
             words = w_sb[:].bitcast(F32)
             gw = gw_pool.tile([P, PASSES, P, 4], BF16, align_bytes=64)
             for c0 in range(0, PASSES, 2):
-                bank = psum_w.tile([P, 2, 2 * P], F32, tag="bank")
+                bank = psum_t.tile([P, 2, 2 * P], F32, tag="bank")
                 for u in range(2):
                     for cc in range(2):
                         first = (c0 + cc) * 2 * P

@@ -20,11 +20,17 @@ PASSES = K // K_PASS
 ROW_TILES = B // P
 TOKEN_TILES = T * ROW_TILES
 HALF = K // 2
-HALF_THROUGH_PSUM = (2, 3, 4, 5, 6, 7)
-SCALAR_EXPERTS = (0, 4, 4, 4, 4, 4, 4, 4)
-
 FLOPS = 2 * T * B * U * K
 BYTES = 4 * T * B * K + 2 * T * U * K + 2 * T * B * V + 4 * T * B * E + 4 * T * B * U
+
+PAIRS = PASSES // 2
+PAIR_V = V // PAIRS
+STEPS = (
+    [(i, c, 1) for i in range(2) for c in range(PAIRS)]
+    + [(i, c, 2) for i in range(2, TOKEN_TILES - 1) for c in (0, 2)]
+    + [(TOKEN_TILES - 1, 0, 2), (TOKEN_TILES - 1, 2, 1), (TOKEN_TILES - 1, 3, 1)]
+)
+SLOT_THROUGH_PSUM = (2, 3, 4, 5, 6, 7)
 
 
 def tile_plelayer_pb_v_kernel(
@@ -36,9 +42,9 @@ def tile_plelayer_pb_v_kernel(
         zt_pool = ctx.enter_context(tc.tile_pool(name="zt", bufs=6))
         w_pool = ctx.enter_context(tc.tile_pool(name="w", bufs=3))
         y_pool = ctx.enter_context(tc.tile_pool(name="y", bufs=3))
-        rows_pool = ctx.enter_context(tc.tile_pool(name="rows", bufs=3))
-        dz_pool = ctx.enter_context(tc.tile_pool(name="dz", bufs=3))
-        dzq_pool = ctx.enter_context(tc.tile_pool(name="dzq", bufs=4))
+        rows_pool = ctx.enter_context(tc.tile_pool(name="rows", bufs=2))
+        dz_pool = ctx.enter_context(tc.tile_pool(name="dz", bufs=2))
+        dzq_pool = ctx.enter_context(tc.tile_pool(name="dzq", bufs=5))
         gw_pool = ctx.enter_context(tc.tile_pool(name="gw", bufs=2))
         wq_pool = ctx.enter_context(tc.tile_pool(name="wq", bufs=2))
         small = ctx.enter_context(tc.tile_pool(name="small", bufs=2))
@@ -50,21 +56,24 @@ def tile_plelayer_pb_v_kernel(
         make_identity(nc, ident[:])
         ident_bf = const.tile([P, P], BF16)
         make_identity(nc, ident_bf[:])
+        ctx.enter_context(tc.manual_schedule())
 
         gate_sb = const.tile([P, TOKEN_TILES, 2 * E], F32)
         g_sb = const.tile([P, TOKEN_TILES, V], BF16)
+        zt_tiles, w_tiles, gws, ys, y_banks, rows, dzs_k, dz_codes = {}, {}, {}, {}, {}, {}, {}, {}
+        w_codes = {}
 
-        def load_zt_half(i, s, pieces):
-            rows = zt[i // ROW_TILES, (i % ROW_TILES) * P : (i % ROW_TILES + 1) * P]
-            rows = rows.rearrange("b v e -> b (v e)")
-            zt_sb = zt_pool.tile([P, HALF], F32)
-            width = HALF // pieces
-            for j in range(pieces):
-                nc.sync.dma_start(
-                    out=zt_sb[:, j * width : (j + 1) * width],
-                    in_=rows[:, s * HALF + j * width : s * HALF + (j + 1) * width],
-                )
-            return zt_sb
+        def load_zt(i, c, n):
+            s = c // 2
+            if (i, s) not in zt_tiles:
+                zt_half = zt_pool.tile([P, HALF], F32)
+                zt_tiles[(i, s)] = zt_half
+            width = K // PAIRS
+            src = zt[i // ROW_TILES, (i % ROW_TILES) * P : (i % ROW_TILES + 1) * P]
+            nc.sync.dma_start(
+                out=zt_tiles[(i, s)][:, (c % 2) * width : (c % 2 + n) * width],
+                in_=src.rearrange("b v e -> b (v e)")[:, c * width : (c + n) * width],
+            )
 
         def load_grad(first, last):
             nc.sync.dma_start(
@@ -72,67 +81,73 @@ def tile_plelayer_pb_v_kernel(
                 in_=grad_out.rearrange("t (n p) v -> p (t n) v", p=P)[:, first:last],
             )
 
-        def load_w(t, n):
-            w_sb = w_pool.tile([P, K], BF16)
+        def load_w(t, n, c, k):
+            if (t, n) not in w_tiles:
+                w_sb = w_pool.tile([P, K], BF16)
+                w_tiles[(t, n)] = w_sb
+            width = K // PAIRS
             nc.sync.dma_start(
-                out=w_sb[:], in_=ew1[t, n * P : (n + 1) * P].rearrange("u v e -> u (v e)")
+                out=w_tiles[(t, n)][:, c * width : (c + k) * width],
+                in_=ew1[t, n * P : (n + 1) * P].rearrange("u v e -> u (v e)")[
+                    :, c * width : (c + k) * width
+                ],
             )
-            return w_sb
 
-        def grad_times_gate(i):
-            y = y_pool.tile([P, 2, 4, V], BF16)
-            for u in range(2):
-                for q in range(4):
-                    e = 4 * (q // 2) + 2 * u + q % 2
-                    if u == 1 and q < SCALAR_EXPERTS[i]:
-                        nc.scalar.activation(
-                            out=y[:, u, q, :], in_=g_sb[:, i], func=COPY, scale=gate_sb[:, i, e : e + 1]
-                        )
-                    else:
-                        nc.vector.tensor_scalar_mul(
-                            out=y[:, u, q, :], in0=g_sb[:, i], scalar1=gate_sb[:, i, e : e + 1]
-                        )
-            return y
+        def y_tile(i):
+            if i not in ys:
+                y = y_pool.tile([P, 2, 4, V], BF16)
+                ys[i] = y
+            return ys[i]
 
-        def y_in_psum(y, u):
+        def grad_times_gate(i, u, q, engine):
+            y = y_tile(i)
+            e = 4 * (q // 2) + 2 * u + q % 2
+            if engine == "scalar":
+                nc.scalar.activation(
+                    out=y[:, u, q, :], in_=g_sb[:, i], func=COPY, scale=gate_sb[:, i, e : e + 1]
+                )
+            else:
+                nc.vector.tensor_scalar_mul(
+                    out=y[:, u, q, :], in0=g_sb[:, i], scalar1=gate_sb[:, i, e : e + 1]
+                )
+
+        def y_in_psum(i, u, s):
             nv = V // 2
             bank = psum_y.tile([P, 4, nv], BF16)
             for m in range(2):
                 nc.tensor.matmul(
                     out=bank[:, 2 * m : 2 * m + 2, :],
                     lhsT=ident_bf[:],
-                    rhs=y[:, u, 2 * m : 2 * m + 2, 0:nv],
+                    rhs=ys[i][:, u, 2 * m : 2 * m + 2, s * nv : (s + 1) * nv],
                     start=True,
                     stop=True,
                 )
-            return bank
+            y_banks[(i, u, s)] = bank
 
-        def masked_rows(y, zt_halves, pieces, banks, after_first_half):
-            rows = rows_pool.tile([P, 2, V, 2, 2], BF16)
-            nv = V // 2 // pieces
-            for s in range(2):
-                for j in range(pieces):
-                    for u in range(2):
-                        v0 = s * (V // 2) + j * nv
-                        if s == 0 and banks:
-                            y_part = banks[u][:]
-                        else:
-                            y_part = y[:, u, :, v0 : v0 + nv]
-                        nc.vector.scalar_tensor_tensor(
-                            out=rows[:, u, v0 : v0 + nv],
-                            in0=zt_halves[s][:, j * nv * E : (j + 1) * nv * E].rearrange(
-                                "p (v a j r) -> p v a j r", a=2, j=2, r=2
-                            )[:, :, :, u, :],
-                            scalar=0.0,
-                            in1=y_part.rearrange("p (a r) v -> p v a r", a=2),
-                            op0=ALU.is_gt,
-                            op1=ALU.mult,
-                        )
-                if s == 0:
-                    after_first_half()
-            return rows
+        def mask(i, c, n):
+            if i not in rows:
+                rows_i = rows_pool.tile([P, 2, V, 2, 2], BF16)
+                rows[i] = rows_i
+            s, v0, nv = c // 2, c * PAIR_V, n * PAIR_V
+            z0 = (c % 2) * (K // PAIRS)
+            for u in range(2):
+                if (i, u, s) in y_banks:
+                    b0 = (c % 2) * PAIR_V
+                    y_part = y_banks[(i, u, s)][:, :, b0 : b0 + nv]
+                else:
+                    y_part = ys[i][:, u, :, v0 : v0 + nv]
+                nc.vector.scalar_tensor_tensor(
+                    out=rows[i][:, u, v0 : v0 + nv],
+                    in0=zt_tiles[(i, s)][:, z0 : z0 + nv * E].rearrange(
+                        "p (v a j r) -> p v a j r", a=2, j=2, r=2
+                    )[:, :, :, u, :],
+                    scalar=0.0,
+                    in1=y_part.rearrange("p (a r) v -> p v a r", a=2),
+                    op0=ALU.is_gt,
+                    op1=ALU.mult,
+                )
 
-        def copy_out(bank, packed, c0):
+        def copy_out(bank, packed, c):
             words = (
                 packed[:]
                 .rearrange("p c x k -> p (c x k)")
@@ -140,60 +155,82 @@ def tile_plelayer_pb_v_kernel(
                 .rearrange("p (x u) -> p x u", u=2)
             )
             nc.scalar.copy(
-                out=words[:, c0 * P : (c0 + 2) * P, :], in_=bank[:].rearrange("p u x -> p x u")
+                out=words[:, 2 * c * P : (2 * c + 2) * P, :], in_=bank[:].rearrange("p u x -> p x u")
             )
 
-        def to_k_major(rows):
-            words = rows[:].rearrange("p u v a r -> p (u v a r)").bitcast(F32)
-            dz = dz_pool.tile([P, PASSES, P, 4], BF16, align_bytes=64)
-            for c0 in range(0, PASSES, 2):
-                bank = psum_t.tile([P, 2, 2 * P], F32, tag="bank")
-                for u in range(2):
-                    for cc in range(2):
-                        first = u * (K // 4) + (c0 + cc) * P
-                        nc.tensor.transpose(
-                            bank[:, u, cc * P : (cc + 1) * P], words[:, first : first + P], ident[:]
-                        )
-                copy_out(bank, dz, c0)
-            return dz
+        def transpose_dz(i, c):
+            words = rows[i][:].rearrange("p u v a r -> p (u v a r)").bitcast(F32)
+            bank = psum_t.tile([P, 2, 2 * P], F32, tag="bank")
+            for u in range(2):
+                for cc in range(2):
+                    first = u * (K // 4) + (2 * c + cc) * P
+                    nc.tensor.transpose(
+                        bank[:, u, cc * P : (cc + 1) * P], words[:, first : first + P], ident[:]
+                    )
+            return bank
 
-        def transpose_w(w_sb):
-            words = w_sb[:].bitcast(F32)
-            gw = gw_pool.tile([P, PASSES, P, 4], BF16, align_bytes=64)
-            for c0 in range(0, PASSES, 2):
-                bank = psum_t.tile([P, 2, 2 * P], F32, tag="bank")
-                for u in range(2):
-                    for cc in range(2):
-                        first = (c0 + cc) * 2 * P
-                        nc.tensor.transpose(
-                            bank[:, u, cc * P : (cc + 1) * P],
-                            words[:, first + u : first + 2 * P : 2],
-                            ident[:],
-                        )
-                copy_out(bank, gw, c0)
-            return gw
+        def copy_dz(bank, i, c):
+            if i not in dzs_k:
+                dz = dz_pool.tile([P, PASSES, P, 4], BF16, align_bytes=64)
+                dzs_k[i] = dz
+            copy_out(bank, dzs_k[i], c)
 
-        def quantise_w(gw, n, wq, ws):
-            for c in range(PASSES):
+        def transpose_w(t, n, c):
+            words = w_tiles[(t, n)][:].bitcast(F32)
+            bank = psum_t.tile([P, 2, 2 * P], F32, tag="bank")
+            for u in range(2):
+                for cc in range(2):
+                    first = (2 * c + cc) * 2 * P
+                    nc.tensor.transpose(
+                        bank[:, u, cc * P : (cc + 1) * P],
+                        words[:, first + u : first + 2 * P : 2],
+                        ident[:],
+                    )
+            return bank
+
+        def copy_w(bank, t, n, c):
+            if (t, n) not in gws:
+                gw = gw_pool.tile([P, PASSES, P, 4], BF16, align_bytes=64)
+                gws[(t, n)] = gw
+            copy_out(bank, gws[(t, n)], c)
+
+        def quantise_w(t, n, c):
+            if t not in w_codes:
+                wq = wq_pool.tile([P, PASSES, U], U32, align_bytes=64)
+                ws = wq_pool.tile([P, PASSES, U], U8, align_bytes=64)
+                w_codes[t] = (wq, ws)
+            wq, ws = w_codes[t]
+            for p in (2 * c, 2 * c + 1):
                 nc.vector.quantize_mx(
-                    out=wq[:, c, n * P : (n + 1) * P].bitcast(E4M3X4),
-                    scales=ws[:, c, n * P : (n + 1) * P],
-                    in_=gw[:, c].rearrange("p u k -> p (u k)"),
+                    out=wq[:, p, n * P : (n + 1) * P].bitcast(E4M3X4),
+                    scales=ws[:, p, n * P : (n + 1) * P],
+                    in_=gws[(t, n)][:, p].rearrange("p u k -> p (u k)"),
                 )
 
-        def quantise_dz(dz, dzq, dzs, q):
-            passes = slice(2 * q, 2 * q + 2)
+        def quantise_dz(i, c, n):
+            if i not in dz_codes:
+                dzq = dzq_pool.tile([P, PASSES, P], U32, align_bytes=64)
+                dzs = dzq_pool.tile([P, PASSES, P], U8, align_bytes=64)
+                dz_codes[i] = (dzq, dzs)
+            dzq, dzs = dz_codes[i]
+            passes = slice(2 * c, 2 * c + 2 * n)
             nc.vector.quantize_mx(
                 out=dzq[:, passes].rearrange("p c b -> p (c b)").bitcast(E5M2X4),
                 scales=dzs[:, passes].rearrange("p c b -> p (c b)"),
-                in_=dz[:, passes].rearrange("p c b k -> p (c b k)"),
+                in_=dzs_k[i][:, passes].rearrange("p c b k -> p (c b k)"),
             )
 
-        def multiply_and_store(i, dzq, dzs, wq, ws):
-            acc = psum_acc.tile([P, U], F32)
-            for c in range(PASSES):
+        accs = {}
+
+        def multiply(i, first, last):
+            if first == 0:
+                acc = psum_acc.tile([P, U], F32)
+                accs[i] = acc
+            dzq, dzs = dz_codes[i]
+            wq, ws = w_codes[i // ROW_TILES]
+            for c in range(first, last):
                 nc.tensor.matmul_mx(
-                    out=acc[:],
+                    out=accs[i][:],
                     lhsT=dzq[:, c, :].bitcast(E5M2X4),
                     lhsT_scale=dzs[:, c, :],
                     rhs=wq[:, c, :].bitcast(E4M3X4),
@@ -201,56 +238,112 @@ def tile_plelayer_pb_v_kernel(
                     start=(c == 0),
                     stop=(c == PASSES - 1),
                 )
+
+        def store(i):
             res = small.tile([P, U], F32)
-            nc.scalar.copy(out=res[:], in_=acc[:])
+            nc.scalar.copy(out=res[:], in_=accs[i][:])
             first = (i % ROW_TILES) * P
             nc.scalar.dma_start(out=out[i // ROW_TILES, first : first + P, :], in_=res[:])
 
-        def new_w_codes():
-            wq = wq_pool.tile([P, PASSES, U], U32, align_bytes=64)
-            ws = wq_pool.tile([P, PASSES, U], U8, align_bytes=64)
-            return wq, ws
+        w_units = [(t, n, c) for t in range(T) for n in range(ROW_TILES) for c in range(PAIRS)]
+        sizes = [2] * 8 + [3] * 4 + [2] * 2
+        w_of_step = [w_units[sum(sizes[:k]) : sum(sizes[: k + 1])] for k in range(len(sizes))]
+        loads = []
+        w_halves = w_units[::2]
+        for k, (i, c, n) in enumerate(STEPS):
+            loads.append(("zt", i, c, n))
+            while w_halves and 32 - 2 * len(w_halves) < sum(sizes[: k + 1 + 0]):
+                t, m, cw = w_halves.pop(0)
+                loads.append(("w", t * ROW_TILES + m, cw, 2))
+            if k == 0:
+                loads.append(("g", 1, 2))
+            if k == 1:
+                loads.append(("g", 2, 4))
+            if k == 7:
+                loads.append(("g", 4, 8))
+        masked, turned = set(), set()
+
+        def issue_loads():
+            while loads:
+                kind, a, b, n = (loads[0] + (0,))[:4]
+                if kind == "zt":
+                    h = 2 * a + b // 2
+                    if h >= 6 and h - 6 not in masked:
+                        return
+                    load_zt(a, b, n)
+                elif kind == "w":
+                    if a >= 3 and a - 3 not in turned:
+                        return
+                    load_w(a // ROW_TILES, a % ROW_TILES, b, n)
+                else:
+                    load_grad(a, b)
+                loads.pop(0)
+
+        y_rows = [(i, q) for i in range(1, TOKEN_TILES) for q in range(4)]
 
         nc.scalar.dma_start(out=gate_sb[:], in_=gate.rearrange("t (n p) e -> p (t n) e", p=P))
         load_grad(0, 1)
-        zt_tiles = {0: [load_zt_half(0, 0, 2), load_zt_half(0, 1, 2)]}
-        load_grad(1, ROW_TILES)
-        zt_tiles[1] = [load_zt_half(1, 0, 1), load_zt_half(1, 1, 1)]
-        w_tiles = {(0, n): load_w(0, n) for n in range(ROW_TILES)}
-        zt_tiles[2] = [load_zt_half(2, 0, 1), load_zt_half(2, 1, 1)]
-        load_grad(ROW_TILES, TOKEN_TILES)
+        issue_loads()
 
-        w_codes = {0: new_w_codes()}
-        ys = {0: grad_times_gate(0)}
-        dzs_k = {0: to_k_major(masked_rows(ys[0], zt_tiles[0], 2, [], lambda: None))}
-        ys[1] = grad_times_gate(1)
-        copies = {}
+        for u in range(2):
+            for q in range(4):
+                grad_times_gate(0, u, q, "vector")
 
-        def copy_next(n):
-            if n in HALF_THROUGH_PSUM:
-                copies[n] = [y_in_psum(ys[n], u) for u in range(2)]
-
-        for i in range(TOKEN_TILES):
-            if i < ROW_TILES:
-                w_tiles[(1, i)] = load_w(1, i)
-            if i + 3 < TOKEN_TILES:
-                zt_tiles[i + 3] = [load_zt_half(i + 3, 0, 1), load_zt_half(i + 3, 1, 1)]
-            if i + 2 < TOKEN_TILES:
-                ys[i + 2] = grad_times_gate(i + 2)
-            if i + 1 < TOKEN_TILES:
-                dzs_k[i + 1] = to_k_major(
-                    masked_rows(
-                        ys[i + 1], zt_tiles[i + 1], 1, copies.get(i + 1, []), lambda: copy_next(i + 2)
-                    )
-                )
-            if i == 0:
-                for n in range(ROW_TILES):
-                    quantise_w(transpose_w(w_tiles[(0, n)]), n, *w_codes[0])
-                w_codes[1] = new_w_codes()
-            dzq = dzq_pool.tile([P, PASSES, P], U32, align_bytes=64)
-            dzs = dzq_pool.tile([P, PASSES, P], U8, align_bytes=64)
-            for q in range(PASSES // 2):
-                quantise_dz(dzs_k[i], dzq, dzs, q)
-            multiply_and_store(i, dzq, dzs, *w_codes[i // ROW_TILES])
-            if i < ROW_TILES:
-                quantise_w(transpose_w(w_tiles[(1, i)]), i, *w_codes[1])
+        todo_mx = []
+        for k in range(len(STEPS) + 1):
+            units = w_of_step[k] if k < len(w_of_step) else []
+            if k < len(STEPS):
+                i, c, n = STEPS[k]
+                mask(i, c, n)
+                if c + n in (2, 4):
+                    masked.add(2 * i + (c + n) // 2 - 1)
+            banks = [transpose_w(*w) for w in units]
+            for b, w in zip(banks, units):
+                copy_w(b, *w)
+                if w[2] == PAIRS - 1:
+                    turned.add(w[0] * ROW_TILES + w[1])
+            products = []
+            for x in range(1 if k < 14 else 2):
+                if todo_mx:
+                    products.append(todo_mx.pop(0))
+            late = k >= len(STEPS) - 3
+            if not late:
+                for product in products:
+                    multiply(*product)
+            if k < len(STEPS):
+                for b in range(c, c + n):
+                    copy_dz(transpose_dz(i, b), i, b)
+                if c + n in (2, 4):
+                    for u in (0,):
+                        if i + 1 in SLOT_THROUGH_PSUM:
+                            y_in_psum(i + 1, u, (c + n) // 2 - 1)
+            if late:
+                for product in products:
+                    multiply(*product)
+            for product in products:
+                if product[2] == PASSES:
+                    store(product[0])
+            if k > 0:
+                pi, pc, pn = STEPS[k - 1]
+                quantise_dz(pi, pc, pn)
+                for w in w_of_step[k - 1] if k <= len(w_of_step) else []:
+                    quantise_w(*w)
+                if k == 8:
+                    todo_mx += [(0, 0, 4), (0, 4, 8), (1, 0, 4), (1, 4, 8)]
+                elif 1 < pi < 4 and pc + pn == PAIRS:
+                    todo_mx += [(pi, 0, 4), (pi, 4, 8)]
+                elif k == 14:
+                    todo_mx += [(x, y, y + 4) for x in range(4, pi + 1) for y in (0, 4) if (x, y) <= (pi, 2 * pc)]
+                elif k > 14:
+                    todo_mx.append((pi, 2 * pc, 2 * (pc + pn)))
+            for r in range(2 if k in (0, 1, 2, 3) or (k < len(STEPS) and n == 2) else 1):
+                if y_rows:
+                    iy, q = y_rows.pop(0)
+                    grad_times_gate(iy, 0, q, "scalar" if iy > 5 else "vector")
+                    grad_times_gate(iy, 1, q, "scalar")
+            issue_loads()
+        while todo_mx:
+            im, first, last = todo_mx.pop(0)
+            multiply(im, first, last)
+            if last == PASSES:
+                store(im)

@@ -23,14 +23,14 @@ HALF = K // 2
 FLOPS = 2 * T * B * U * K
 BYTES = 4 * T * B * K + 2 * T * U * K + 2 * T * B * V + 4 * T * B * E + 4 * T * B * U
 
-PAIRS = PASSES // 2
-PAIR_V = V // PAIRS
+PASS_V = V // PASSES
 STEPS = (
-    [(i, c, 1) for i in range(2) for c in range(PAIRS)]
-    + [(i, c, 2) for i in range(2, TOKEN_TILES - 1) for c in (0, 2)]
-    + [(TOKEN_TILES - 1, 0, 2), (TOKEN_TILES - 1, 2, 1), (TOKEN_TILES - 1, 3, 1)]
+    [(i, c, 2) for i in range(2) for c in range(0, PASSES, 2)]
+    + [(i, c, 4) for i in range(2, TOKEN_TILES - 1) for c in (0, 4)]
+    + [(TOKEN_TILES - 1, c, n) for c, n in ((0, 4), (4, 2), (6, 1), (7, 1))]
 )
-SLOT_THROUGH_PSUM = (2, 3, 4, 5, 6, 7)
+SLOT_THROUGH_PSUM = (1, 2, 3, 4, 5, 6)
+W_PER_STEP = [0] + [2] * 8 + [3] * 4 + [2] * 2
 
 
 def tile_plelayer_pb_v_kernel(
@@ -45,7 +45,7 @@ def tile_plelayer_pb_v_kernel(
         rows_pool = ctx.enter_context(tc.tile_pool(name="rows", bufs=2))
         dz_pool = ctx.enter_context(tc.tile_pool(name="dz", bufs=2))
         dzq_pool = ctx.enter_context(tc.tile_pool(name="dzq", bufs=5))
-        gw_pool = ctx.enter_context(tc.tile_pool(name="gw", bufs=2))
+        gw_pool = ctx.enter_context(tc.tile_pool(name="gw", bufs=4))
         wq_pool = ctx.enter_context(tc.tile_pool(name="wq", bufs=2))
         small = ctx.enter_context(tc.tile_pool(name="small", bufs=2))
         psum_t = ctx.enter_context(tc.psum_pool(name="psum_t", bufs=4))
@@ -61,18 +61,17 @@ def tile_plelayer_pb_v_kernel(
         gate_sb = const.tile([P, TOKEN_TILES, 2 * E], F32)
         g_sb = const.tile([P, TOKEN_TILES, V], BF16)
         zt_tiles, w_tiles, gws, ys, y_banks, rows, dzs_k, dz_codes = {}, {}, {}, {}, {}, {}, {}, {}
-        w_codes = {}
+        w_codes, accs = {}, {}
 
         def load_zt(i, c, n):
-            s = c // 2
+            s = c // 4
             if (i, s) not in zt_tiles:
                 zt_half = zt_pool.tile([P, HALF], F32)
                 zt_tiles[(i, s)] = zt_half
-            width = K // PAIRS
             src = zt[i // ROW_TILES, (i % ROW_TILES) * P : (i % ROW_TILES + 1) * P]
             nc.sync.dma_start(
-                out=zt_tiles[(i, s)][:, (c % 2) * width : (c % 2 + n) * width],
-                in_=src.rearrange("b v e -> b (v e)")[:, c * width : (c + n) * width],
+                out=zt_tiles[(i, s)][:, (c % 4) * K_PASS : (c % 4 + n) * K_PASS],
+                in_=src.rearrange("b v e -> b (v e)")[:, c * K_PASS : (c + n) * K_PASS],
             )
 
         def load_grad(first, last):
@@ -81,59 +80,53 @@ def tile_plelayer_pb_v_kernel(
                 in_=grad_out.rearrange("t (n p) v -> p (t n) v", p=P)[:, first:last],
             )
 
-        def load_w(t, n, c, k):
-            if (t, n) not in w_tiles:
-                w_sb = w_pool.tile([P, K], BF16)
-                w_tiles[(t, n)] = w_sb
-            width = K // PAIRS
+        def load_w(t, q):
+            w_sb = w_pool.tile([P, ROW_TILES, 2 * K_PASS], BF16)
             nc.sync.dma_start(
-                out=w_tiles[(t, n)][:, c * width : (c + k) * width],
-                in_=ew1[t, n * P : (n + 1) * P].rearrange("u v e -> u (v e)")[
-                    :, c * width : (c + k) * width
+                out=w_sb[:],
+                in_=ew1[t].rearrange("(n p) v e -> p n (v e)", p=P)[
+                    :, :, 2 * q * K_PASS : 2 * (q + 1) * K_PASS
                 ],
             )
+            w_tiles[(t, q)] = w_sb
 
-        def y_tile(i):
+        def grad_times_gate(i, u, q, engine):
             if i not in ys:
                 y = y_pool.tile([P, 2, 4, V], BF16)
                 ys[i] = y
-            return ys[i]
-
-        def grad_times_gate(i, u, q, engine):
-            y = y_tile(i)
+            y_row = ys[i][:, u, q, :]
             e = 4 * (q // 2) + 2 * u + q % 2
             if engine == "scalar":
                 nc.scalar.activation(
-                    out=y[:, u, q, :], in_=g_sb[:, i], func=COPY, scale=gate_sb[:, i, e : e + 1]
+                    out=y_row, in_=g_sb[:, i], func=COPY, scale=gate_sb[:, i, e : e + 1]
                 )
             else:
                 nc.vector.tensor_scalar_mul(
-                    out=y[:, u, q, :], in0=g_sb[:, i], scalar1=gate_sb[:, i, e : e + 1]
+                    out=y_row, in0=g_sb[:, i], scalar1=gate_sb[:, i, e : e + 1]
                 )
 
-        def y_in_psum(i, u, s):
+        def y_in_psum(i, s):
             nv = V // 2
             bank = psum_y.tile([P, 4, nv], BF16)
             for m in range(2):
                 nc.tensor.matmul(
                     out=bank[:, 2 * m : 2 * m + 2, :],
                     lhsT=ident_bf[:],
-                    rhs=ys[i][:, u, 2 * m : 2 * m + 2, s * nv : (s + 1) * nv],
+                    rhs=ys[i][:, 0, 2 * m : 2 * m + 2, s * nv : (s + 1) * nv],
                     start=True,
                     stop=True,
                 )
-            y_banks[(i, u, s)] = bank
+            y_banks[(i, s)] = bank
 
         def mask(i, c, n):
             if i not in rows:
                 rows_i = rows_pool.tile([P, 2, V, 2, 2], BF16)
                 rows[i] = rows_i
-            s, v0, nv = c // 2, c * PAIR_V, n * PAIR_V
-            z0 = (c % 2) * (K // PAIRS)
+            s, v0, nv = c // 4, c * PASS_V, n * PASS_V
+            z0 = (c % 4) * K_PASS
             for u in range(2):
-                if (i, u, s) in y_banks:
-                    b0 = (c % 2) * PAIR_V
-                    y_part = y_banks[(i, u, s)][:, :, b0 : b0 + nv]
+                if u == 0 and (i, s) in y_banks:
+                    y_part = y_banks[(i, s)][:, :, (c % 4) * PASS_V : (c % 4) * PASS_V + nv]
                 else:
                     y_part = ys[i][:, u, :, v0 : v0 + nv]
                 nc.vector.scalar_tensor_tensor(
@@ -147,65 +140,55 @@ def tile_plelayer_pb_v_kernel(
                     op1=ALU.mult,
                 )
 
-        def copy_out(bank, packed, c):
-            words = (
-                packed[:]
-                .rearrange("p c x k -> p (c x k)")
-                .bitcast(F32)
-                .rearrange("p (x u) -> p x u", u=2)
-            )
-            nc.scalar.copy(
-                out=words[:, 2 * c * P : (2 * c + 2) * P, :], in_=bank[:].rearrange("p u x -> p x u")
-            )
+        def copy_out(bank, words):
+            nc.scalar.copy(out=words, in_=bank.rearrange("p u x -> p x u"))
 
-        def transpose_dz(i, c):
-            words = rows[i][:].rearrange("p u v a r -> p (u v a r)").bitcast(F32)
-            bank = psum_t.tile([P, 2, 2 * P], F32, tag="bank")
-            for u in range(2):
-                for cc in range(2):
-                    first = u * (K // 4) + (2 * c + cc) * P
-                    nc.tensor.transpose(
-                        bank[:, u, cc * P : (cc + 1) * P], words[:, first : first + P], ident[:]
-                    )
-            return bank
-
-        def copy_dz(bank, i, c):
+        def turn_dz(i, c, n):
             if i not in dzs_k:
                 dz = dz_pool.tile([P, PASSES, P, 4], BF16, align_bytes=64)
                 dzs_k[i] = dz
-            copy_out(bank, dzs_k[i], c)
-
-        def transpose_w(t, n, c):
-            words = w_tiles[(t, n)][:].bitcast(F32)
+            words = rows[i][:].rearrange("p u v a r -> p (u v a r)").bitcast(F32)
             bank = psum_t.tile([P, 2, 2 * P], F32, tag="bank")
             for u in range(2):
-                for cc in range(2):
-                    first = (2 * c + cc) * 2 * P
+                for cc in range(n):
+                    first = u * (K // 4) + (c + cc) * P
                     nc.tensor.transpose(
-                        bank[:, u, cc * P : (cc + 1) * P],
+                        bank[:, u, cc * P : (cc + 1) * P], words[:, first : first + P], ident[:]
+                    )
+            packed = dzs_k[i][:].rearrange("p c x k -> p (c x k)").bitcast(F32)
+            packed = packed.rearrange("p (x u) -> p x u", u=2)
+            copy_out(bank[:, :, 0 : n * P], packed[:, c * P : (c + n) * P, :])
+
+        def turn_w(t, c, m):
+            bank = psum_t.tile([P, 2, 2 * P], F32, tag="bank")
+            for u in range(2):
+                for nn in range(2):
+                    words = w_tiles[(t, c // 2)][:, 2 * m + nn, :].bitcast(F32)
+                    first = c % 2 * 2 * P
+                    nc.tensor.transpose(
+                        bank[:, u, nn * P : (nn + 1) * P],
                         words[:, first + u : first + 2 * P : 2],
                         ident[:],
                     )
-            return bank
+            if m == 0:
+                gw = gw_pool.tile([P, U, 4], BF16, align_bytes=64)
+                gws[(t, c)] = gw
+            packed = gws[(t, c)][:].rearrange("p x k -> p (x k)").bitcast(F32)
+            packed = packed.rearrange("p (x u) -> p x u", u=2)
+            copy_out(bank[:], packed[:, 2 * m * P : 2 * (m + 1) * P, :])
 
-        def copy_w(bank, t, n, c):
-            if (t, n) not in gws:
-                gw = gw_pool.tile([P, PASSES, P, 4], BF16, align_bytes=64)
-                gws[(t, n)] = gw
-            copy_out(bank, gws[(t, n)], c)
-
-        def quantise_w(t, n, c):
+        def quantise_w(t, c):
             if t not in w_codes:
                 wq = wq_pool.tile([P, PASSES, U], U32, align_bytes=64)
                 ws = wq_pool.tile([P, PASSES, U], U8, align_bytes=64)
                 w_codes[t] = (wq, ws)
             wq, ws = w_codes[t]
-            for p in (2 * c, 2 * c + 1):
-                nc.vector.quantize_mx(
-                    out=wq[:, p, n * P : (n + 1) * P].bitcast(E4M3X4),
-                    scales=ws[:, p, n * P : (n + 1) * P],
-                    in_=gws[(t, n)][:, p].rearrange("p u k -> p (u k)"),
-                )
+            nc.vector.quantize_mx(
+                out=wq[:, c].bitcast(E4M3X4),
+                scales=ws[:, c],
+                in_=gws[(t, c)][:].rearrange("p x k -> p (x k)"),
+            )
+            w_done.append((t, c))
 
         def quantise_dz(i, c, n):
             if i not in dz_codes:
@@ -213,31 +196,27 @@ def tile_plelayer_pb_v_kernel(
                 dzs = dzq_pool.tile([P, PASSES, P], U8, align_bytes=64)
                 dz_codes[i] = (dzq, dzs)
             dzq, dzs = dz_codes[i]
-            passes = slice(2 * c, 2 * c + 2 * n)
             nc.vector.quantize_mx(
-                out=dzq[:, passes].rearrange("p c b -> p (c b)").bitcast(E5M2X4),
-                scales=dzs[:, passes].rearrange("p c b -> p (c b)"),
-                in_=dzs_k[i][:, passes].rearrange("p c b k -> p (c b k)"),
+                out=dzq[:, c : c + n].rearrange("p c b -> p (c b)").bitcast(E5M2X4),
+                scales=dzs[:, c : c + n].rearrange("p c b -> p (c b)"),
+                in_=dzs_k[i][:, c : c + n].rearrange("p c b k -> p (c b k)"),
             )
 
-        accs = {}
-
-        def multiply(i, first, last):
-            if first == 0:
+        def multiply(i, c):
+            if c == 0:
                 acc = psum_acc.tile([P, U], F32)
                 accs[i] = acc
             dzq, dzs = dz_codes[i]
             wq, ws = w_codes[i // ROW_TILES]
-            for c in range(first, last):
-                nc.tensor.matmul_mx(
-                    out=accs[i][:],
-                    lhsT=dzq[:, c, :].bitcast(E5M2X4),
-                    lhsT_scale=dzs[:, c, :],
-                    rhs=wq[:, c, :].bitcast(E4M3X4),
-                    rhs_scale=ws[:, c, :],
-                    start=(c == 0),
-                    stop=(c == PASSES - 1),
-                )
+            nc.tensor.matmul_mx(
+                out=accs[i][:],
+                lhsT=dzq[:, c, :].bitcast(E5M2X4),
+                lhsT_scale=dzs[:, c, :],
+                rhs=wq[:, c, :].bitcast(E4M3X4),
+                rhs_scale=ws[:, c, :],
+                start=(c == 0),
+                stop=(c == PASSES - 1),
+            )
 
         def store(i):
             res = small.tile([P, U], F32)
@@ -245,105 +224,103 @@ def tile_plelayer_pb_v_kernel(
             first = (i % ROW_TILES) * P
             nc.scalar.dma_start(out=out[i // ROW_TILES, first : first + P, :], in_=res[:])
 
-        w_units = [(t, n, c) for t in range(T) for n in range(ROW_TILES) for c in range(PAIRS)]
-        sizes = [2] * 8 + [3] * 4 + [2] * 2
-        w_of_step = [w_units[sum(sizes[:k]) : sum(sizes[: k + 1])] for k in range(len(sizes))]
+        w_units = [(t, c, m) for t in range(T) for c in range(PASSES) for m in range(2)]
+        w_of_step = [
+            w_units[sum(W_PER_STEP[:k]) : sum(W_PER_STEP[: k + 1])] for k in range(len(W_PER_STEP))
+        ]
+        w_loads = [("w", t, q) for t in range(T) for q in range(PASSES // 2)]
         loads = []
-        w_halves = w_units[::2]
         for k, (i, c, n) in enumerate(STEPS):
             loads.append(("zt", i, c, n))
-            while w_halves and 32 - 2 * len(w_halves) < sum(sizes[: k + 1 + 0]):
-                t, m, cw = w_halves.pop(0)
-                loads.append(("w", t * ROW_TILES + m, cw, 2))
             if k == 0:
-                loads.append(("g", 1, 2))
-            if k == 1:
-                loads.append(("g", 2, 4))
+                loads.append(("grad", 2, ROW_TILES))
             if k == 7:
-                loads.append(("g", 4, 8))
-        masked, turned = set(), set()
+                loads.append(("grad", ROW_TILES, TOKEN_TILES))
+            if k % 2 == 0 and w_loads:
+                loads.extend(w_loads[:1])
+                w_loads = w_loads[1:]
+        masked, turned = [], []
 
         def issue_loads():
             while loads:
-                kind, a, b, n = (loads[0] + (0,))[:4]
+                kind, place = loads[0][0], loads[0][1:]
                 if kind == "zt":
-                    h = 2 * a + b // 2
-                    if h >= 6 and h - 6 not in masked:
+                    half = 2 * place[0] + place[1] // 4
+                    if half >= 6 and half - 6 not in masked:
                         return
-                    load_zt(a, b, n)
+                    load_zt(*place)
                 elif kind == "w":
-                    if a >= 3 and a - 3 not in turned:
+                    number = place[0] * PASSES // 2 + place[1]
+                    if number >= 3 and number - 3 not in turned:
                         return
-                    load_w(a // ROW_TILES, a % ROW_TILES, b, n)
+                    load_w(*place)
                 else:
-                    load_grad(a, b)
+                    load_grad(*place)
                 loads.pop(0)
 
-        y_rows = [(i, q) for i in range(1, TOKEN_TILES) for q in range(4)]
+        y_rows = [(i, q) for i in range(2, TOKEN_TILES) for q in range(4)]
 
         nc.scalar.dma_start(out=gate_sb[:], in_=gate.rearrange("t (n p) e -> p (t n) e", p=P))
-        load_grad(0, 1)
+        load_grad(0, 2)
         issue_loads()
+        for q in range(4):
+            grad_times_gate(0, 0, q, "vector")
+        for q in range(4):
+            grad_times_gate(0, 1, q, "scalar" if q > 1 else "vector")
+        for q in range(4):
+            grad_times_gate(1, 0, q, "vector")
+            grad_times_gate(1, 1, q, "scalar")
 
-        for u in range(2):
-            for q in range(4):
-                grad_times_gate(0, u, q, "vector")
-
-        todo_mx = []
+        dz_done, w_done, multiplied, finished = [], [], [], 0
         for k in range(len(STEPS) + 1):
             units = w_of_step[k] if k < len(w_of_step) else []
+            at_end = k >= len(STEPS) - 1
             if k < len(STEPS):
                 i, c, n = STEPS[k]
                 mask(i, c, n)
-                if c + n in (2, 4):
-                    masked.add(2 * i + (c + n) // 2 - 1)
-            banks = [transpose_w(*w) for w in units]
-            for b, w in zip(banks, units):
-                copy_w(b, *w)
-                if w[2] == PAIRS - 1:
-                    turned.add(w[0] * ROW_TILES + w[1])
-            products = []
-            for x in range(1 if k < 14 else 2):
-                if todo_mx:
-                    products.append(todo_mx.pop(0))
-            late = k >= len(STEPS) - 3
-            if not late:
+                if (c + n) % 4 == 0:
+                    masked.append(2 * i + c // 4)
+            for t, cw, m in units:
+                turn_w(t, cw, m)
+                if cw % 2 == 1 and m == 1:
+                    turned.append((t * PASSES + cw) // 2)
+            products = [
+                (ip, cp)
+                for ip in range(finished, min(finished + 2, TOKEN_TILES))
+                for cp in range(PASSES)
+                if (ip, cp) in dz_done and (ip // ROW_TILES, cp) in w_done and (ip, cp) not in multiplied
+            ][: 6 if k >= 8 else 3]
+            multiplied.extend(products)
+            if not at_end:
                 for product in products:
                     multiply(*product)
             if k < len(STEPS):
-                for b in range(c, c + n):
-                    copy_dz(transpose_dz(i, b), i, b)
-                if c + n in (2, 4):
-                    for u in (0,):
-                        if i + 1 in SLOT_THROUGH_PSUM:
-                            y_in_psum(i + 1, u, (c + n) // 2 - 1)
-            if late:
+                for cc in range(c, c + n, 2):
+                    turn_dz(i, cc, min(2, c + n - cc))
+                if (c + n) % 4 == 0 and i + 1 in SLOT_THROUGH_PSUM:
+                    y_in_psum(i + 1, c // 4)
+            if at_end:
                 for product in products:
                     multiply(*product)
             for product in products:
-                if product[2] == PASSES:
+                if product[1] == PASSES - 1:
                     store(product[0])
-            if k > 0:
-                pi, pc, pn = STEPS[k - 1]
-                quantise_dz(pi, pc, pn)
-                for w in w_of_step[k - 1] if k <= len(w_of_step) else []:
-                    quantise_w(*w)
-                if k == 8:
-                    todo_mx += [(0, 0, 4), (0, 4, 8), (1, 0, 4), (1, 4, 8)]
-                elif 1 < pi < 4 and pc + pn == PAIRS:
-                    todo_mx += [(pi, 0, 4), (pi, 4, 8)]
-                elif k == 14:
-                    todo_mx += [(x, y, y + 4) for x in range(4, pi + 1) for y in (0, 4) if (x, y) <= (pi, 2 * pc)]
-                elif k > 14:
-                    todo_mx.append((pi, 2 * pc, 2 * (pc + pn)))
-            for r in range(2 if k in (0, 1, 2, 3) or (k < len(STEPS) and n == 2) else 1):
+                    finished += 1
+            for r in range(2 if n == 4 else 1):
                 if y_rows:
                     iy, q = y_rows.pop(0)
-                    grad_times_gate(iy, 0, q, "scalar" if iy > 5 else "vector")
+                    grad_times_gate(iy, 0, q, "scalar" if iy > 6 else "vector")
                     grad_times_gate(iy, 1, q, "scalar")
+            if k > 0:
+                for unit in w_of_step[k - 1] if 0 <= k - 1 < len(w_of_step) else []:
+                    if unit[2] == 1:
+                        quantise_w(*unit[:2])
+                pi, pc, pn = STEPS[k - 1]
+                quantise_dz(pi, pc, pn)
+                dz_done.extend((pi, cp) for cp in range(pc, pc + pn))
             issue_loads()
-        while todo_mx:
-            im, first, last = todo_mx.pop(0)
-            multiply(im, first, last)
-            if last == PASSES:
-                store(im)
+        for ip in range(finished, TOKEN_TILES):
+            for cp in range(PASSES):
+                if (ip, cp) not in multiplied:
+                    multiply(ip, cp)
+            store(ip)

@@ -58,7 +58,7 @@ def tile_plelayer_pb_v_kernel(
         make_identity(nc, ident_bf[:])
         ctx.enter_context(tc.manual_schedule())
 
-        gate_sb = const.tile([P, TOKEN_TILES, 2 * E], F32)
+        gate_sb = const.tile([P, TOKEN_TILES, E], F32)
         g_sb = const.tile([P, TOKEN_TILES, V], BF16)
         zt_tiles, w_tiles, gws, ys, y_banks, rows, dzs_k, dz_codes = {}, {}, {}, {}, {}, {}, {}, {}
         w_codes, accs = {}, {}
@@ -72,6 +72,12 @@ def tile_plelayer_pb_v_kernel(
             nc.sync.dma_start(
                 out=zt_tiles[(i, s)][:, (c % 4) * K_PASS : (c % 4 + n) * K_PASS],
                 in_=src.rearrange("b v e -> b (v e)")[:, c * K_PASS : (c + n) * K_PASS],
+            )
+
+        def load_gate(first, last, queue):
+            queue.dma_start(
+                out=gate_sb[:, first:last],
+                in_=gate.rearrange("t (n p) e -> p (t n) e", p=P)[:, first:last, 0:E],
             )
 
         def load_grad(first, last):
@@ -219,26 +225,38 @@ def tile_plelayer_pb_v_kernel(
             )
 
         def store(i):
-            res = small.tile([P, U], F32)
-            nc.scalar.copy(out=res[:], in_=accs[i][:])
-            first = (i % ROW_TILES) * P
-            nc.scalar.dma_start(out=out[i // ROW_TILES, first : first + P, :], in_=res[:])
+            rows_out = out[i // ROW_TILES, (i % ROW_TILES) * P : (i % ROW_TILES + 1) * P, :]
+            if i < TOKEN_TILES - 1:
+                res = small.tile([P, U], F32)
+                nc.scalar.copy(out=res[:], in_=accs[i][:])
+                nc.scalar.dma_start(out=rows_out, in_=res[:])
+            else:
+                res_0 = small.tile([P, U // 2], F32)
+                res_1 = small.tile([P, U // 2], F32)
+                nc.scalar.copy(out=res_0[:], in_=accs[i][:, 0 : U // 2])
+                nc.scalar.dma_start(out=rows_out[:, 0 : U // 2], in_=res_0[:])
+                nc.vector.tensor_copy(out=res_1[:], in_=accs[i][:, U // 2 : U])
+                nc.sync.dma_start(out=rows_out[:, U // 2 : U], in_=res_1[:])
 
         w_units = [(t, c, m) for t in range(T) for c in range(PASSES) for m in range(2)]
         w_of_step = [
             w_units[sum(W_PER_STEP[:k]) : sum(W_PER_STEP[: k + 1])] for k in range(len(W_PER_STEP))
         ]
-        w_loads = [("w", t, q) for t in range(T) for q in range(PASSES // 2)]
+        slices_of_step = [
+            [(t, c // 2) for t, c, m in units if c % 2 == 0 and m == 0] for units in w_of_step
+        ]
         loads = []
         for k, (i, c, n) in enumerate(STEPS):
             loads.append(("zt", i, c, n))
             if k == 0:
+                loads.append(("grad", 1, 2))
+                loads.append(("gate", 1, TOKEN_TILES))
+            if k == 1:
                 loads.append(("grad", 2, ROW_TILES))
             if k == 7:
                 loads.append(("grad", ROW_TILES, TOKEN_TILES))
-            if k % 2 == 0 and w_loads:
-                loads.extend(w_loads[:1])
-                w_loads = w_loads[1:]
+            for slice_next in slices_of_step[k if k == 0 else k + 1 : k + 1 + 1]:
+                loads.extend(("w",) + place for place in slice_next)
         masked, turned = [], []
 
         def issue_loads():
@@ -254,22 +272,33 @@ def tile_plelayer_pb_v_kernel(
                     if number >= 3 and number - 3 not in turned:
                         return
                     load_w(*place)
+                elif kind == "gate":
+                    load_gate(*place, nc.sync)
                 else:
                     load_grad(*place)
                 loads.pop(0)
 
-        y_rows = [(i, q) for i in range(2, TOKEN_TILES) for q in range(4)]
+        y_first = [[(1, 0, q, "vector") for q in range(4)]]
+        first_rows = [
+            (i, 0, q, "vector") for i in range(2, TOKEN_TILES - 0) for q in range(4)
+        ]
+        y_first += [first_rows[0:2]] + [[row] for row in first_rows[2:]]
+        y_second = [[(i, 1, q, "scalar")] for i in range(1, TOKEN_TILES - 0) for q in range(4)]
+        y_second += [
+            [(i, 0, q, "scalar"), (i, 1, q, "scalar")]
+            for i in range(TOKEN_TILES - 0, TOKEN_TILES)
+            for q in range(4)
+        ]
 
-        nc.scalar.dma_start(out=gate_sb[:], in_=gate.rearrange("t (n p) e -> p (t n) e", p=P))
-        load_grad(0, 2)
+        load_gate(0, 1, nc.scalar)
+        load_grad(0, 1)
         issue_loads()
         for q in range(4):
             grad_times_gate(0, 0, q, "vector")
         for q in range(4):
-            grad_times_gate(0, 1, q, "scalar" if q > 1 else "vector")
+            grad_times_gate(0, 1, q, "scalar" if q > 2 else "vector")
         for q in range(4):
-            grad_times_gate(1, 0, q, "vector")
-            grad_times_gate(1, 1, q, "scalar")
+            grad_times_gate(*y_second.pop(0)[0])
 
         dz_done, w_done, multiplied, finished = [], [], [], 0
         for k in range(len(STEPS) + 1):
@@ -289,7 +318,7 @@ def tile_plelayer_pb_v_kernel(
                 for ip in range(finished, min(finished + 2, TOKEN_TILES))
                 for cp in range(PASSES)
                 if (ip, cp) in dz_done and (ip // ROW_TILES, cp) in w_done and (ip, cp) not in multiplied
-            ][: 6 if k >= 8 else 3]
+            ][: 5 if k >= 8 else 2]
             multiplied.extend(products)
             if not at_end:
                 for product in products:
@@ -306,11 +335,12 @@ def tile_plelayer_pb_v_kernel(
                 if product[1] == PASSES - 1:
                     store(product[0])
                     finished += 1
-            for r in range(2 if n == 4 else 1):
-                if y_rows:
-                    iy, q = y_rows.pop(0)
-                    grad_times_gate(iy, 0, q, "scalar" if iy > 6 else "vector")
-                    grad_times_gate(iy, 1, q, "scalar")
+            if k < len(STEPS):
+                for q in range(c // 2, (c + n) // 2):
+                    for y_list in (y_first, y_second):
+                        if y_list:
+                            for row in y_list.pop(0):
+                                grad_times_gate(*row)
             if k > 0:
                 for unit in w_of_step[k - 1] if 0 <= k - 1 < len(w_of_step) else []:
                     if unit[2] == 1:

@@ -25,12 +25,11 @@ BYTES = 4 * T * B * K + 2 * T * U * K + 2 * T * B * V + 4 * T * B * E + 4 * T * 
 
 PASS_V = V // PASSES
 STEPS = (
-    [(i, c, 2) for i in range(2) for c in range(0, PASSES, 2)]
-    + [(i, c, 4) for i in range(2, TOKEN_TILES - 1) for c in (0, 4)]
+    [(0, c, 2) for c in range(0, PASSES, 2)]
+    + [(i, c, 4) for i in range(1, TOKEN_TILES - 1) for c in (0, 4)]
     + [(TOKEN_TILES - 1, c, n) for c, n in ((0, 4), (4, 2), (6, 1), (7, 1))]
 )
-SLOT_THROUGH_PSUM = (1, 2, 3, 4, 5, 6)
-W_PER_STEP = [0] + [2] * 8 + [3] * 4 + [2] * 2
+W_PER_STEP = [0, 0, 0, 0, 0, 3, 3, 3, 3, 4, 4, 4, 4, 4]
 
 
 def tile_plelayer_pb_v_kernel(
@@ -47,20 +46,17 @@ def tile_plelayer_pb_v_kernel(
         dzq_pool = ctx.enter_context(tc.tile_pool(name="dzq", bufs=5))
         gw_pool = ctx.enter_context(tc.tile_pool(name="gw", bufs=4))
         wq_pool = ctx.enter_context(tc.tile_pool(name="wq", bufs=2))
-        small = ctx.enter_context(tc.tile_pool(name="small", bufs=2))
-        psum_t = ctx.enter_context(tc.psum_pool(name="psum_t", bufs=4))
-        psum_y = ctx.enter_context(tc.psum_pool(name="psum_y", bufs=2))
-        psum_acc = ctx.enter_context(tc.psum_pool(name="psum_acc", bufs=2))
+        small = ctx.enter_context(tc.tile_pool(name="small", bufs=3))
+        psum_t = ctx.enter_context(tc.psum_pool(name="psum_t", bufs=5))
+        psum_acc = ctx.enter_context(tc.psum_pool(name="psum_acc", bufs=3))
 
         ident = const.tile([P, P], F32)
         make_identity(nc, ident[:])
-        ident_bf = const.tile([P, P], BF16)
-        make_identity(nc, ident_bf[:])
         ctx.enter_context(tc.manual_schedule())
 
         gate_sb = const.tile([P, TOKEN_TILES, E], F32)
         g_sb = const.tile([P, TOKEN_TILES, V], BF16)
-        zt_tiles, w_tiles, gws, ys, y_banks, rows, dzs_k, dz_codes = {}, {}, {}, {}, {}, {}, {}, {}
+        zt_tiles, w_tiles, gws, ys, rows, dzs_k, dz_codes = {}, {}, {}, {}, {}, {}, {}
         w_codes, accs = {}, {}
 
         def load_zt(i, c, n):
@@ -111,19 +107,6 @@ def tile_plelayer_pb_v_kernel(
                     out=y_row, in0=g_sb[:, i], scalar1=gate_sb[:, i, e : e + 1]
                 )
 
-        def y_in_psum(i, s):
-            nv = V // 2
-            bank = psum_y.tile([P, 4, nv], BF16)
-            for m in range(2):
-                nc.tensor.matmul(
-                    out=bank[:, 2 * m : 2 * m + 2, :],
-                    lhsT=ident_bf[:],
-                    rhs=ys[i][:, 0, 2 * m : 2 * m + 2, s * nv : (s + 1) * nv],
-                    start=True,
-                    stop=True,
-                )
-            y_banks[(i, s)] = bank
-
         def mask(i, c, n):
             if i not in rows:
                 rows_i = rows_pool.tile([P, 2, V, 2, 2], BF16)
@@ -131,10 +114,7 @@ def tile_plelayer_pb_v_kernel(
             s, v0, nv = c // 4, c * PASS_V, n * PASS_V
             z0 = (c % 4) * K_PASS
             for u in range(2):
-                if u == 0 and (i, s) in y_banks:
-                    y_part = y_banks[(i, s)][:, :, (c % 4) * PASS_V : (c % 4) * PASS_V + nv]
-                else:
-                    y_part = ys[i][:, u, :, v0 : v0 + nv]
+                y_part = ys[i][:, u, :, v0 : v0 + nv]
                 nc.vector.scalar_tensor_tensor(
                     out=rows[i][:, u, v0 : v0 + nv],
                     in0=zt_tiles[(i, s)][:, z0 : z0 + nv * E].rearrange(
@@ -224,7 +204,10 @@ def tile_plelayer_pb_v_kernel(
                 stop=(c == PASSES - 1),
             )
 
+        stored = []
+
         def store(i):
+            stored.append(i)
             rows_out = out[i // ROW_TILES, (i % ROW_TILES) * P : (i % ROW_TILES + 1) * P, :]
             if i < TOKEN_TILES - 1:
                 res = small.tile([P, U], F32)
@@ -253,9 +236,9 @@ def tile_plelayer_pb_v_kernel(
                 loads.append(("gate", 1, TOKEN_TILES))
             if k == 1:
                 loads.append(("grad", 2, ROW_TILES))
-            if k == 7:
+            if k == 4:
                 loads.append(("grad", ROW_TILES, TOKEN_TILES))
-            for slice_next in slices_of_step[k if k == 0 else k + 1 : k + 1 + 1]:
+            for slice_next in slices_of_step[k if k == 0 else k + 0 : k + 0 + 1]:
                 loads.extend(("w",) + place for place in slice_next)
         masked, turned = [], []
 
@@ -300,7 +283,7 @@ def tile_plelayer_pb_v_kernel(
         for q in range(4):
             grad_times_gate(*y_second.pop(0)[0])
 
-        dz_done, w_done, multiplied, finished = [], [], [], 0
+        dz_done, w_done, multiplied, finished = [], [], [], []
         for k in range(len(STEPS) + 1):
             units = w_of_step[k] if k < len(w_of_step) else []
             at_end = k >= len(STEPS) - 1
@@ -315,10 +298,13 @@ def tile_plelayer_pb_v_kernel(
                     turned.append((t * PASSES + cw) // 2)
             products = [
                 (ip, cp)
-                for ip in range(finished, min(finished + 2, TOKEN_TILES))
+                for t in range(T)
                 for cp in range(PASSES)
-                if (ip, cp) in dz_done and (ip // ROW_TILES, cp) in w_done and (ip, cp) not in multiplied
-            ][: 5 if k >= 8 else 2]
+                for ip in range(t * ROW_TILES, (t + 1) * ROW_TILES)
+                if (ip, cp) in dz_done and (t, cp) in w_done and (ip, cp) not in multiplied
+                and (ip < ROW_TILES or ip - ROW_TILES in stored)
+                and ip < len(stored) + 3
+            ][: 8 if k >= 10 else 4]
             multiplied.extend(products)
             if not at_end:
                 for product in products:
@@ -326,15 +312,15 @@ def tile_plelayer_pb_v_kernel(
             if k < len(STEPS):
                 for cc in range(c, c + n, 2):
                     turn_dz(i, cc, min(2, c + n - cc))
-                if (c + n) % 4 == 0 and i + 1 in SLOT_THROUGH_PSUM:
-                    y_in_psum(i + 1, c // 4)
             if at_end:
                 for product in products:
                     multiply(*product)
             for product in products:
                 if product[1] == PASSES - 1:
-                    store(product[0])
-                    finished += 1
+                    finished.append(product[0])
+            for i_done in finished[: 1 if k < len(STEPS) - 3 else 4]:
+                store(i_done)
+                finished.remove(i_done)
             if k < len(STEPS):
                 for q in range(c // 2, (c + n) // 2):
                     for y_list in (y_first, y_second):
@@ -349,8 +335,11 @@ def tile_plelayer_pb_v_kernel(
                 quantise_dz(pi, pc, pn)
                 dz_done.extend((pi, cp) for cp in range(pc, pc + pn))
             issue_loads()
-        for ip in range(finished, TOKEN_TILES):
+        for ip in range(TOKEN_TILES):
             for cp in range(PASSES):
                 if (ip, cp) not in multiplied:
                     multiply(ip, cp)
+                    if cp == PASSES - 1:
+                        finished.append(ip)
+        for ip in finished:
             store(ip)

@@ -29,7 +29,7 @@ STEPS = (
     + [(i, c, 4) for i in range(1, TOKEN_TILES - 1) for c in (0, 4)]
     + [(TOKEN_TILES - 1, c, n) for c, n in ((0, 4), (4, 2), (6, 1), (7, 1))]
 )
-W_PER_STEP = [0, 0, 0, 0, 0, 3, 3, 3, 3, 4, 4, 4, 4, 4]
+W_PER_STEP = [0] * 5 + [4] * 4 + [3] * 5 + [1]
 
 
 def tile_plelayer_pb_v_kernel(
@@ -266,7 +266,7 @@ def tile_plelayer_pb_v_kernel(
             (i, 0, q, "vector") for i in range(2, TOKEN_TILES - 0) for q in range(4)
         ]
         y_first += [first_rows[0:2]] + [[row] for row in first_rows[2:]]
-        y_second = [[(i, 1, q, "scalar")] for i in range(1, TOKEN_TILES - 0) for q in range(4)]
+        y_second = [[(i, 1, q, "scalar" if i < 5 or q > 1 else "vector")] for i in range(1, TOKEN_TILES - 0) for q in range(4)]
         y_second += [
             [(i, 0, q, "scalar"), (i, 1, q, "scalar")]
             for i in range(TOKEN_TILES - 0, TOKEN_TILES)

from contextlib import ExitStack

import concourse.mybir as mybir
from concourse.masks import make_identity

F32 = mybir.dt.float32
BF16 = mybir.dt.bfloat16
U32 = mybir.dt.uint32
U8 = mybir.dt.uint8
E4M3X4 = mybir.dt.float8_e4m3fn_x4
E5M2X4 = mybir.dt.float8_e5m2_x4
ALU = mybir.AluOpType
COPY = mybir.ActivationFunctionType.Copy

P = 128
T, B, U, V, E = 2, 512, 512, 512, 8
K = V * E
K_PASS = 4 * P
PASSES = K // K_PASS
ROW_TILES = B // P
TOKEN_TILES = T * ROW_TILES
HALF = K // 2
FLOPS = 2 * T * B * U * K
BYTES = 4 * T * B * K + 2 * T * U * K + 2 * T * B * V + 4 * T * B * E + 4 * T * B * U

PASS_V = V // PASSES
STEPS = (
    [(0, c, 2) for c in range(0, PASSES, 2)]
    + [(i, c, 4) for i in range(1, TOKEN_TILES - 1) for c in (0, 4)]
    + [(TOKEN_TILES - 1, c, n) for c, n in ((0, 4), (4, 2), (6, 1), (7, 1))]
)
W_PER_STEP = [0] * 5 + [4] * 4 + [3] * 5 + [1]


def tile_plelayer_pb_v_kernel(
    tc, task_h, share_h, ews1, ebs1, ew1, eb1, gate_pre1, gb1, zt, gate, grad_out, out
):
    nc = tc.nc
    with ExitStack() as ctx:
        const = ctx.enter_context(tc.tile_pool(name="const", bufs=1))
        zt_pool = ctx.enter_context(tc.tile_pool(name="zt", bufs=6))
        w_pool = ctx.enter_context(tc.tile_pool(name="w", bufs=3))
        y_pool = ctx.enter_context(tc.tile_pool(name="y", bufs=3))
        rows_pool = ctx.enter_context(tc.tile_pool(name="rows", bufs=2))
        dz_pool = ctx.enter_context(tc.tile_pool(name="dz", bufs=2))
        dzq_pool = ctx.enter_context(tc.tile_pool(name="dzq", bufs=5))
        gw_pool = ctx.enter_context(tc.tile_pool(name="gw", bufs=4))
        wq_pool = ctx.enter_context(tc.tile_pool(name="wq", bufs=2))
        small = ctx.enter_context(tc.tile_pool(name="small", bufs=3))
        psum_t = ctx.enter_context(tc.psum_pool(name="psum_t", bufs=5))
        psum_acc = ctx.enter_context(tc.psum_pool(name="psum_acc", bufs=3))

        ident = const.tile([P, P], F32)
        make_identity(nc, ident[:])
        ctx.enter_context(tc.manual_schedule())

        gate_sb = const.tile([P, TOKEN_TILES, E], F32)
        g_sb = const.tile([P, TOKEN_TILES, V], BF16)
        zt_tiles, w_tiles, gws, ys, rows, dzs_k, dz_codes = {}, {}, {}, {}, {}, {}, {}
        w_codes, accs = {}, {}

        def load_zt(i, c, n):
            s = c // 4
            if (i, s) not in zt_tiles:
                zt_half = zt_pool.tile([P, HALF], F32)
                zt_tiles[(i, s)] = zt_half
            src = zt[i // ROW_TILES, (i % ROW_TILES) * P : (i % ROW_TILES + 1) * P]
            nc.sync.dma_start(
                out=zt_tiles[(i, s)][:, (c % 4) * K_PASS : (c % 4 + n) * K_PASS],
                in_=src.rearrange("b v e -> b (v e)")[:, c * K_PASS : (c + n) * K_PASS],
            )

        def load_gate(first, last, queue):
            queue.dma_start(
                out=gate_sb[:, first:last],
                in_=gate.rearrange("t (n p) e -> p (t n) e", p=P)[:, first:last, 0:E],
            )

        def load_grad(first, last):
            nc.sync.dma_start(
                out=g_sb[:, first:last],
                in_=grad_out.rearrange("t (n p) v -> p (t n) v", p=P)[:, first:last],
            )

        def load_w(t, q):
            w_sb = w_pool.tile([P, ROW_TILES, 2 * K_PASS], BF16)
            nc.sync.dma_start(
                out=w_sb[:],
                in_=ew1[t].rearrange("(n p) v e -> p n (v e)", p=P)[
                    :, :, 2 * q * K_PASS : 2 * (q + 1) * K_PASS
                ],
            )
            w_tiles[(t, q)] = w_sb

        def grad_times_gate(i, u, q, engine):
            if i not in ys:
                y = y_pool.tile([P, 2, 4, V], BF16)
                ys[i] = y
            y_row = ys[i][:, u, q, :]
            e = 4 * (q // 2) + 2 * u + q % 2
            if engine == "scalar":
                nc.scalar.activation(
                    out=y_row, in_=g_sb[:, i], func=COPY, scale=gate_sb[:, i, e : e + 1]
                )
            else:
                nc.vector.tensor_scalar_mul(
                    out=y_row, in0=g_sb[:, i], scalar1=gate_sb[:, i, e : e + 1]
                )

        def mask(i, c, n):
            if i not in rows:
                rows_i = rows_pool.tile([P, 2, V, 2, 2], BF16)
                rows[i] = rows_i
            s, v0, nv = c // 4, c * PASS_V, n * PASS_V
            z0 = (c % 4) * K_PASS
            for u in range(2):
                y_part = ys[i][:, u, :, v0 : v0 + nv]
                nc.vector.scalar_tensor_tensor(
                    out=rows[i][:, u, v0 : v0 + nv],
                    in0=zt_tiles[(i, s)][:, z0 : z0 + nv * E].rearrange(
                        "p (v a j r) -> p v a j r", a=2, j=2, r=2
                    )[:, :, :, u, :],
                    scalar=0.0,
                    in1=y_part.rearrange("p (a r) v -> p v a r", a=2),
                    op0=ALU.is_gt,
                    op1=ALU.mult,
                )

        def copy_out(bank, words):
            nc.scalar.copy(out=words, in_=bank.rearrange("p u x -> p x u"))

        def turn_dz(i, c, n):
            if i not in dzs_k:
                dz = dz_pool.tile([P, PASSES, P, 4], BF16, align_bytes=64)
                dzs_k[i] = dz
            words = rows[i][:].rearrange("p u v a r -> p (u v a r)").bitcast(F32)
            bank = psum_t.tile([P, 2, 2 * P], F32, tag="bank")
            for u in range(2):
                for cc in range(n):
                    first = u * (K // 4) + (c + cc) * P
                    nc.tensor.transpose(
                        bank[:, u, cc * P : (cc + 1) * P], words[:, first : first + P], ident[:]
                    )
            packed = dzs_k[i][:].rearrange("p c x k -> p (c x k)").bitcast(F32)
            packed = packed.rearrange("p (x u) -> p x u", u=2)
            copy_out(bank[:, :, 0 : n * P], packed[:, c * P : (c + n) * P, :])

        def turn_w(t, c, m):
            bank = psum_t.tile([P, 2, 2 * P], F32, tag="bank")
            for u in range(2):
                for nn in range(2):
                    words = w_tiles[(t, c // 2)][:, 2 * m + nn, :].bitcast(F32)
                    first = c % 2 * 2 * P
                    nc.tensor.transpose(
                        bank[:, u, nn * P : (nn + 1) * P],
                        words[:, first + u : first + 2 * P : 2],
                        ident[:],
                    )
            if m == 0:
                gw = gw_pool.tile([P, U, 4], BF16, align_bytes=64)
                gws[(t, c)] = gw
            packed = gws[(t, c)][:].rearrange("p x k -> p (x k)").bitcast(F32)
            packed = packed.rearrange("p (x u) -> p x u", u=2)
            copy_out(bank[:], packed[:, 2 * m * P : 2 * (m + 1) * P, :])

        def quantise_w(t, c):
            if t not in w_codes:
                wq = wq_pool.tile([P, PASSES, U], U32, align_bytes=64)
                ws = wq_pool.tile([P, PASSES, U], U8, align_bytes=64)
                w_codes[t] = (wq, ws)
            wq, ws = w_codes[t]
            nc.vector.quantize_mx(
                out=wq[:, c].bitcast(E4M3X4),
                scales=ws[:, c],
                in_=gws[(t, c)][:].rearrange("p x k -> p (x k)"),
            )
            w_done.append((t, c))

        def quantise_dz(i, c, n):
            if i not in dz_codes:
                dzq = dzq_pool.tile([P, PASSES, P], U32, align_bytes=64)
                dzs = dzq_pool.tile([P, PASSES, P], U8, align_bytes=64)
                dz_codes[i] = (dzq, dzs)
            dzq, dzs = dz_codes[i]
            nc.vector.quantize_mx(
                out=dzq[:, c : c + n].rearrange("p c b -> p (c b)").bitcast(E5M2X4),
                scales=dzs[:, c : c + n].rearrange("p c b -> p (c b)"),
                in_=dzs_k[i][:, c : c + n].rearrange("p c b k -> p (c b k)"),
            )

        def multiply(i, c):
            if c == 0:
                acc = psum_acc.tile([P, U], F32)
                accs[i] = acc
            dzq, dzs = dz_codes[i]
            wq, ws = w_codes[i // ROW_TILES]
            nc.tensor.matmul_mx(
                out=accs[i][:],
                lhsT=dzq[:, c, :].bitcast(E5M2X4),
                lhsT_scale=dzs[:, c, :],
                rhs=wq[:, c, :].bitcast(E4M3X4),
                rhs_scale=ws[:, c, :],
                start=(c == 0),
                stop=(c == PASSES - 1),
            )

        stored = []

        def store(i):
            stored.append(i)
            rows_out = out[i // ROW_TILES, (i % ROW_TILES) * P : (i % ROW_TILES + 1) * P, :]
            if i < TOKEN_TILES - 1:
                res = small.tile([P, U], F32)
                nc.scalar.copy(out=res[:], in_=accs[i][:])
                nc.scalar.dma_start(out=rows_out, in_=res[:])
            else:
                res_0 = small.tile([P, U // 2], F32)
                res_1 = small.tile([P, U // 2], F32)
                nc.scalar.copy(out=res_0[:], in_=accs[i][:, 0 : U // 2])
                nc.scalar.dma_start(out=rows_out[:, 0 : U // 2], in_=res_0[:])
                nc.vector.tensor_copy(out=res_1[:], in_=accs[i][:, U // 2 : U])
                nc.sync.dma_start(out=rows_out[:, U // 2 : U], in_=res_1[:])

        w_units = [(t, c, m) for t in range(T) for c in range(PASSES) for m in range(2)]
        w_of_step = [
            w_units[sum(W_PER_STEP[:k]) : sum(W_PER_STEP[: k + 1])] for k in range(len(W_PER_STEP))
        ]
        slices_of_step = [
            [(t, c // 2) for t, c, m in units if c % 2 == 0 and m == 0] for units in w_of_step
        ]
        loads = []
        for k, (i, c, n) in enumerate(STEPS):
            loads.append(("zt", i, c, n))
            if k == 0:
                loads.append(("grad", 1, 2))
                loads.append(("gate", 1, TOKEN_TILES))
            if k == 1:
                loads.append(("grad", 2, ROW_TILES))
            if k == 4:
                loads.append(("grad", ROW_TILES, TOKEN_TILES))
            for slice_next in slices_of_step[k if k == 0 else k + 0 : k + 0 + 1]:
                loads.extend(("w",) + place for place in slice_next)
        masked, turned = [], []

        def issue_loads():
            while loads:
                kind, place = loads[0][0], loads[0][1:]
                if kind == "zt":
                    half = 2 * place[0] + place[1] // 4
                    if half >= 6 and half - 6 not in masked:
                        return
                    load_zt(*place)
                elif kind == "w":
                    number = place[0] * PASSES // 2 + place[1]
                    if number >= 3 and number - 3 not in turned:
                        return
                    load_w(*place)
                elif kind == "gate":
                    load_gate(*place, nc.sync)
                else:
                    load_grad(*place)
                loads.pop(0)

        y_first = [[(1, 0, q, "vector") for q in range(4)]]
        first_rows = [
            (i, 0, q, "vector") for i in range(2, TOKEN_TILES - 0) for q in range(4)
        ]
        y_first += [first_rows[0:2]] + [[row] for row in first_rows[2:]]
        y_second = [[(i, 1, q, "scalar" if i < 5 or q > 1 else "vector")] for i in range(1, TOKEN_TILES - 0) for q in range(4)]
        y_second += [
            [(i, 0, q, "scalar"), (i, 1, q, "scalar")]
            for i in range(TOKEN_TILES - 0, TOKEN_TILES)
            for q in range(4)
        ]

        load_gate(0, 1, nc.scalar)
        load_grad(0, 1)
        issue_loads()
        for q in range(4):
            grad_times_gate(0, 0, q, "vector")
        for q in range(4):
            grad_times_gate(0, 1, q, "scalar" if q > 2 else "vector")
        for q in range(4):
            grad_times_gate(*y_second.pop(0)[0])

        dz_done, w_done, multiplied, finished = [], [], [], []
        for k in range(len(STEPS) + 1):
            units = w_of_step[k] if k < len(w_of_step) else []
            at_end = k >= len(STEPS) - 1
            if k < len(STEPS):
                i, c, n = STEPS[k]
                mask(i, c, n)
                if (c + n) % 4 == 0:
                    masked.append(2 * i + c // 4)
            for t, cw, m in units:
                turn_w(t, cw, m)
                if cw % 2 == 1 and m == 1:
                    turned.append((t * PASSES + cw) // 2)
            products = [
                (ip, cp)
                for t in range(T)
                for cp in range(PASSES)
                for ip in range(t * ROW_TILES, (t + 1) * ROW_TILES)
                if (ip, cp) in dz_done and (t, cp) in w_done and (ip, cp) not in multiplied
                and (ip < ROW_TILES or ip - ROW_TILES in stored)
                and ip < len(stored) + 3
            ][: 8 if k >= 10 else 4]
            multiplied.extend(products)
            if not at_end:
                for product in products:
                    multiply(*product)
            if k < len(STEPS):
                for cc in range(c, c + n, 2):
                    turn_dz(i, cc, min(2, c + n - cc))
            if at_end:
                for product in products:
                    multiply(*product)
            for product in products:
                if product[1] == PASSES - 1:
                    finished.append(product[0])
            for i_done in finished[: 1 if k < len(STEPS) - 3 else 4]:
                store(i_done)
                finished.remove(i_done)
            if k < len(STEPS):
                for q in range(c // 2, (c + n) // 2):
                    for y_list in (y_first, y_second):
                        if y_list:
                            for row in y_list.pop(0):
                                grad_times_gate(*row)
            if k > 0:
                for unit in w_of_step[k - 1] if 0 <= k - 1 < len(w_of_step) else []:
                    if unit[2] == 1:
                        quantise_w(*unit[:2])
                pi, pc, pn = STEPS[k - 1]
                quantise_dz(pi, pc, pn)
                dz_done.extend((pi, cp) for cp in range(pc, pc + pn))
            issue_loads()
        for ip in range(TOKEN_TILES):
            for cp in range(PASSES):
                if (ip, cp) not in multiplied:
                    multiply(ip, cp)
                    if cp == PASSES - 1:
                        finished.append(ip)
        for ip in finished:
            store(ip)
